import numpy as np
import ml_dtypes


def mxq(x, axis, fmt="e4m3"):
    dtype, down = {"e4m3": (ml_dtypes.float8_e4m3fn, 7), "e5m2": (ml_dtypes.float8_e5m2, 14)}[fmt]
    v = np.moveaxis(np.asarray(x, np.float32).astype(ml_dtypes.bfloat16).astype(np.float64), axis, -1)
    blocks = v.reshape(v.shape[:-1] + (-1, 32))
    amax = np.abs(blocks).max(-1, keepdims=True)
    byte = np.maximum(np.where(amax > 0, np.frexp(amax)[1] - 1 + 127, 0) - down, 1)
    scale = np.exp2(byte - 127.0)
    codes = (blocks / scale).astype(np.float32).astype(dtype).astype(np.float64)
    return np.moveaxis((codes * scale).reshape(v.shape), -1, axis)


WIDE = False


def mx_kscale(k):
    if not WIDE:
        return np.ones(k)
    levels = np.array([10, -10, 5, -5, 0])
    a = np.random.permutation(np.resize(levels, k // 512 * 4)).reshape(k // 512, 4)
    idx = np.arange(k)
    return np.exp2(a[idx // 512, idx % 128 // 32])


BF16 = ml_dtypes.bfloat16


def bf(x):
    return np.asarray(x, np.float32).astype(BF16)


def f64(x):
    return np.asarray(x).astype(np.float64)


B, IN_DIM, MEM = 8192, 256, 256
DIN = MEM + IN_DIM
MIN_TS, MAX_TS, EPS = 0.1, 10.0, 1e-6


def sigmoid(v):
    return 1.0 / (1.0 + np.exp(-v))


def setup_inputs():
    s = mx_kscale(DIN)[MEM:]
    r = np.concatenate([np.ones(MEM), s])
    return {"x": bf(np.random.standard_normal((B, IN_DIM)) * s),
            "h": bf(np.random.standard_normal((B, MEM))),
            "h_candidate": bf(np.tanh(0.7 * np.random.standard_normal((B, MEM)))),
            "Wd": bf(np.random.standard_normal((DIN, MEM)) * 1.3 / np.sqrt(DIN) / r[:, None]),
            "bd": bf(np.random.standard_normal(MEM) * 0.5),
            "Wu": bf(np.random.standard_normal((DIN, MEM)) * 1.3 / np.sqrt(DIN) / r[:, None]),
            "bu": bf(np.random.standard_normal(MEM) * 0.5)}


def reference(x, h, h_candidate, Wd, bd, Wu, bu):
    h = f64(h)
    cq = mxq(np.concatenate([h, f64(x)], axis=-1), 1, "e4m3")
    decay = sigmoid((cq @ mxq(f64(Wd), 0, "e4m3")) + f64(bd))
    update = sigmoid((cq @ mxq(f64(Wu), 0, "e4m3")) + f64(bu))
    decay = MIN_TS + (MAX_TS - MIN_TS) * decay + EPS
    new_h = (1.0 - update) * (h / decay) + update * f64(h_candidate)
    h_norm = np.maximum(np.sqrt(np.square(h).sum(-1, keepdims=True)), EPS)
    nh_norm = np.maximum(np.sqrt(np.square(new_h).sum(-1, keepdims=True)), 1e-12)
    return new_h / nh_norm * h_norm

@@ -1,0 +1,247 @@
+import math
+from contextlib import ExitStack
+
+import concourse.mybir as mybir
+from concourse.masks import make_identity
+
+F32 = mybir.dt.float32
+BF16 = mybir.dt.bfloat16
+U32 = mybir.dt.uint32
+U8 = mybir.dt.uint8
+FP8X4 = mybir.dt.float8_e4m3fn_x4
+ALU = mybir.AluOpType
+ACT = mybir.ActivationFunctionType
+
+P = 128
+B, IN_DIM, MEM = 8192, 256, 256
+DIN = MEM + IN_DIM
+NT = B // P
+GT = 4
+NG = NT // GT
+FLOPS = 2 * B * DIN * 2 * MEM
+
+PIN = True
+
+A_LOW = 0.1 + 1e-6
+SPAN = 10.0 - 0.1
+KAPPA = (A_LOW + SPAN) / A_LOW
+LN_KAPPA = math.log(KAPPA)
+BETA = SPAN / (A_LOW * (A_LOW + SPAN))
+RHO = A_LOW / SPAN
+INV_BETA = 1.0 / BETA
+CLAMP_M2 = (1e-12 / BETA) * (1e-12 / BETA)
+CLAMP_H2 = 1e-6 * 1e-6
+
+CHUNKS = [1, 1, 2, 2, 2, 2, 2, 2, 2]
+
+
+def tile_liquidmemorycell_pb_t_kernel(tc, x, h, h_candidate, Wd, bd, Wu, bu, out):
+    nc = tc.nc
+    assert sum(CHUNKS) == NG
+    with ExitStack() as ctx:
+        const = ctx.enter_context(tc.tile_pool(name="const", bufs=1))
+        inp = ctx.enter_context(tc.tile_pool(name="inp", bufs=1))
+        work = ctx.enter_context(tc.tile_pool(name="work", bufs=2))
+        res = ctx.enter_context(tc.tile_pool(name="res", bufs=3))
+        psum = ctx.enter_context(tc.psum_pool(name="psum", bufs=1))
+
+        hv = h.rearrange("(p j) f -> p j f", j=NT)
+        xv = x.rearrange("(p j) f -> p j f", j=NT)
+        cv = h_candidate.rearrange("(p j) f -> p j f", j=NT)
+        ov = out.rearrange("(p j) f -> p j f", j=NT)
+
+        warm = const.tile([P, 1], F32, name="warm")
+        nc.vector.memset(warm[:], 0.0)
+        warm2 = const.tile([P, 1], F32, name="warm2")
+        nc.scalar.activation(out=warm2[:], in_=warm[:], func=ACT.Sigmoid)
+        ident = const.tile([P, P], F32, name="ident")
+        make_identity(nc, ident[:])
+        neg_half = const.tile([P, GT], F32, name="neg_half")
+        nc.gpsimd.memset(neg_half[:], -0.5)
+        pos_half = const.tile([P, GT], F32, name="pos_half")
+        nc.gpsimd.memset(pos_half[:], 0.5)
+        brows = const.tile([P, P], BF16, name="brows")
+        nc.gpsimd.memset(brows[:], 0.0)
+
+        c_of = {}
+        hc_of = {}
+        wraw = const.tile([P, 4, 2 * MEM], BF16, name="wraw")
+        g0 = 0
+        for ci, ng in enumerate(CHUNKS):
+            nt = ng * GT
+            j0 = g0 * GT
+            ctile = inp.tile([P, nt * DIN], BF16, name="c%d" % ci)
+            c3 = ctile[:].rearrange("p (j f) -> p j f", f=DIN)
+            nc.sync.dma_start(out=c3[:, :, 0:MEM], in_=hv[:, j0:j0 + nt, :])
+            nc.sync.dma_start(out=c3[:, :, MEM:DIN], in_=xv[:, j0:j0 + nt, :])
+            if ci == 0:
+                nc.sync.dma_start(out=wraw[:, :, 0:MEM], in_=Wd.rearrange("(p j) w -> p j w", j=4))
+                nc.sync.dma_start(out=wraw[:, :, MEM:2 * MEM], in_=Wu.rearrange("(p j) w -> p j w", j=4))
+                nc.sync.dma_start(out=brows[0:2, :], in_=bd.rearrange("(r c) -> r c", c=P))
+                nc.sync.dma_start(out=brows[2:4, :], in_=bu.rearrange("(r c) -> r c", c=P))
+            hctile = inp.tile([P, nt * MEM], BF16, name="hc%d" % ci)
+            hc3 = hctile[:].rearrange("p (j f) -> p j f", f=MEM)
+            nc.sync.dma_start(out=hc3, in_=cv[:, j0:j0 + nt, :])
+            cw = ctile[:].bitcast(F32).rearrange("p (j w u) -> p j u w", u=2, w=P)
+            for k in range(ng):
+                c_of[g0 + k] = (c3[:, k * GT:(k + 1) * GT, :], cw[:, k * GT:(k + 1) * GT, :, :])
+                hc_of[g0 + k] = hc3[:, k * GT:(k + 1) * GT, :]
+            g0 += ng
+
+        if PIN:
+            ctx.enter_context(tc.manual_schedule())
+
+        st = {}
+        bias = const.tile([P, 4], F32, name="bias")
+        wcodes = const.tile([P, 2 * MEM], U32, name="wcodes", align_bytes=64)
+        wscl = const.tile([P, 2 * MEM], U8, name="wscl", align_bytes=64)
+
+        def prep_weights():
+            wgrp = const.tile([P, 2 * MEM, 4], BF16, name="wgrp", align_bytes=64)
+            nc.vector.tensor_copy(out=wgrp[:], in_=wraw[:].rearrange("p j w -> p w j"))
+            ident_bf = const.tile([P, P], BF16, name="ident_bf")
+            nc.vector.tensor_copy(out=ident_bf[:], in_=ident[:])
+            nc.vector.quantize_mx(out=wcodes[:].bitcast(FP8X4), scales=wscl[:],
+                                  in_=wgrp[:].rearrange("p w j -> p (w j)"))
+            bps = psum.tile([P, P], BF16, tag="D", name="bps")
+            nc.tensor.transpose(bps[:], brows[:], ident_bf[:])
+            nc.vector.tensor_scalar(out=bias[:, 0:2], in0=bps[:, 0:2], scalar1=-1.0,
+                                    scalar2=-LN_KAPPA, op0=ALU.mult, op1=ALU.add)
+            nc.vector.tensor_copy(out=bias[:, 2:4], in_=bps[:, 2:4])
+
+        def stage_a(g):
+            cw = c_of[g][1]
+            banks = []
+            for half in range(2):
+                ct = psum.tile([P, 2, 2 * P], F32, tag="ct%d" % half, name="ct")
+                for jl in range(2):
+                    for u in range(2):
+                        nc.tensor.transpose(ct[:, u, P * jl:P * (jl + 1)], cw[:, 2 * half + jl, u, :], ident[:])
+                banks.append(ct)
+            st[("ct", g)] = banks
+
+        def stage_b(g):
+            grp = work.tile([P, GT * P * 4], BF16, tag="grp", name="grp", align_bytes=64)
+            gw = grp[:].bitcast(F32).rearrange("p (r u) -> p r u", u=2)
+            for half in range(2):
+                ct = st[("ct", g)][half]
+                nc.scalar.copy(out=gw[:, 2 * P * half:2 * P * (half + 1), :],
+                               in_=ct[:].rearrange("p u r -> p r u"))
+            st[("grp", g)] = grp
+
+        def stage_c(g):
+            codes = work.tile([P, GT * P], U32, tag="codes", name="codes", align_bytes=64)
+            scl = work.tile([P, GT * P], U8, tag="scl", name="scl", align_bytes=64)
+            nc.vector.quantize_mx(out=codes[:].bitcast(FP8X4), scales=scl[:], in_=st[("grp", g)][:])
+            st[("codes", g)] = (codes, scl)
+
+        def stage_d(g):
+            codes, scl = st[("codes", g)]
+            zs = []
+            for b in range(4):
+                z = psum.tile([P, GT * P], F32, tag="z%d" % b, name="z")
+                nc.tensor.matmul_mx(out=z[:], lhsT=wcodes[:, P * b:P * (b + 1)].bitcast(FP8X4),
+                                    lhsT_scale=wscl[:, P * b:P * (b + 1)],
+                                    rhs=codes[:].bitcast(FP8X4), rhs_scale=scl[:],
+                                    start=True, stop=True)
+                zs.append(z)
+            st[("z", g)] = zs
+
+        def stage_e(g):
+            sT = work.tile([P, 4, GT * P], F32, tag="sT", name="sT")
+            for b in range(4):
+                nc.scalar.activation(out=sT[:, b, :], in_=st[("z", g)][b][:], func=ACT.Sigmoid,
+                                     bias=bias[:, b:b + 1], scale=(-1.0 if b < 2 else 1.0))
+            st[("sT", g)] = sT
+
+        def stage_f(g, pair, which):
+            sT = st[("sT", g)]
+            bank = psum.tile([P, 2, MEM], F32, tag=("D" if which == 0 else "U"), name="bank")
+            for jl in range(2):
+                for bb in range(2):
+                    r0 = P * (2 * pair + jl)
+                    nc.tensor.transpose(bank[:, jl, P * bb:P * (bb + 1)],
+                                        sT[:, 2 * which + bb, r0:r0 + P], ident[:])
+            st[("DU", g, pair, which)] = bank
+
+        def stage_g(g, pair):
+            if pair == 0:
+                mt = res.tile([P, GT, MEM], F32, tag="m", name="mt")
+                st[("m", g)] = mt
+            mt = st[("m", g)]
+            js = slice(2 * pair, 2 * pair + 2)
+            q = work.tile([P, 2, MEM], F32, tag="q", name="q")
+            t = work.tile([P, 2, MEM], F32, tag="t", name="t")
+            nc.vector.scalar_tensor_tensor(out=q[:], in0=st[("DU", g, pair, 0)][:], scalar=RHO,
+                                           in1=c_of[g][0][:, js, 0:MEM], op0=ALU.add, op1=ALU.mult)
+            nc.vector.scalar_tensor_tensor(out=t[:], in0=hc_of[g][:, js, :], scalar=INV_BETA,
+                                           in1=q[:], op0=ALU.mult, op1=ALU.subtract)
+            nc.vector.tensor_tensor(out=t[:], in0=t[:], in1=st[("DU", g, pair, 1)][:], op=ALU.mult)
+            nc.vector.tensor_tensor(out=mt[:, js, :], in0=t[:], in1=q[:], op=ALU.add)
+
+        def stage_h(g, pair):
+            if pair == 0:
+                ssm = const.tile([P, GT], F32, name="ssm%d" % g)
+                st[("ssm", g)] = ssm
+            ssm = st[("ssm", g)]
+            for jl in range(2 * pair, 2 * pair + 2):
+                junk = work.tile([P, MEM], BF16, tag="junk", name="junk")
+                nc.scalar.activation(out=junk[:], in_=st[("m", g)][:, jl, :], func=ACT.Square,
+                                     accum_out=ssm[:, jl:jl + 1])
+
+        def stage_k(g):
+            ssh = const.tile([P, GT], F32, name="ssh%d" % g)
+            for jl in range(GT):
+                junk = work.tile([P, MEM], BF16, tag="junk", name="junk")
+                nc.scalar.activation(out=junk[:], in_=c_of[g][0][:, jl, 0:MEM], func=ACT.Square,
+                                     accum_out=ssh[:, jl:jl + 1])
+            sh = const.tile([P, GT], F32, name="sh%d" % g)
+            nc.gpsimd.tensor_scalar_max(out=sh[:], in0=ssh[:], scalar1=CLAMP_H2)
+            nc.gpsimd.tensor_tensor(out=sh[:], in0=sh[:], in1=pos_half[:], op=ALU.pow)
+            st[("sh", g)] = sh
+
+        def stage_i(g):
+            rs = const.tile([P, GT], F32, name="rs%d" % g)
+            nc.gpsimd.tensor_scalar_max(out=rs[:], in0=st[("ssm", g)][:], scalar1=CLAMP_M2)
+            nc.gpsimd.tensor_tensor(out=rs[:], in0=rs[:], in1=neg_half[:], op=ALU.pow)
+            nc.gpsimd.tensor_tensor(out=rs[:], in0=rs[:], in1=st[("sh", g)][:], op=ALU.mult)
+            st[("rs", g)] = rs
+
+        def stage_j(g):
+            o = res.tile([P, GT, MEM], F32, tag="o", name="o")
+            for jl in range(GT):
+                nc.vector.tensor_scalar(out=o[:, jl, :], in0=st[("m", g)][:, jl, :],
+                                        scalar1=st[("rs", g)][:, jl:jl + 1], scalar2=None, op0=ALU.mult)
+            nc.sync.dma_start(out=ov[:, g * GT:(g + 1) * GT, :], in_=o[:])
+
+        def ok(g):
+            return 0 <= g < NG
+
+        for it in range(-3, NG + 1):
+            if it == -2:
+                prep_weights()
+            if ok(it + 3):
+                stage_a(it + 3)
+            if ok(it - 1):
+                stage_h(it - 1, 1)
+                stage_i(it - 1)
+            if ok(it + 1):
+                stage_e(it + 1)
+            if ok(it):
+                stage_g(it, 0)
+                stage_f(it, 1, 0)
+                stage_f(it, 1, 1)
+                stage_h(it, 0)
+            if ok(it + 2):
+                stage_c(it + 2)
+                stage_d(it + 2)
+            if ok(it):
+                stage_g(it, 1)
+            if ok(it + 1):
+                stage_f(it + 1, 0, 0)
+                stage_f(it + 1, 0, 1)
+            if ok(it + 3):
+                stage_k(it + 3)
+                stage_b(it + 3)
+            if ok(it - 1):
+                stage_j(it - 1)

@@ -148,36 +148,53 @@ def tile_liquidmemorycell_pb_t_kernel(tc, x, h, h_candidate, Wd, bd, Wu, bu, out
             st[("z", g)] = zs
 
         def stage_e(g):
-            sT = work.tile([P, 4, GT * P], F32, tag="sT", name="sT")
-            for b in range(4):
-                nc.scalar.activation(out=sT[:, b, :], in_=st[("z", g)][b][:], func=ACT.Sigmoid,
-                                     bias=bias[:, b:b + 1], scale=(-1.0 if b < 2 else 1.0))
-            st[("sT", g)] = sT
+            halves = []
+            for which in range(2):
+                sT = work.tile([P, 2, GT * P], F32, tag="sT%d" % which, name="sT")
+                for bb in range(2):
+                    b = 2 * which + bb
+                    nc.scalar.activation(out=sT[:, bb, :], in_=st[("z", g)][b][:], func=ACT.Sigmoid,
+                                         bias=bias[:, b:b + 1], scale=(-1.0 if which == 0 else 1.0))
+                halves.append(sT)
+            st[("sT", g)] = halves
 
-        def stage_f(g, pair, which):
-            sT = st[("sT", g)]
+        def stage_f(n, which):
+            g, pair = n // 2, n % 2
+            sT = st[("sT", g)][which]
             bank = psum.tile([P, 2, MEM], F32, tag=("D" if which == 0 else "U"), name="bank")
             for jl in range(2):
                 for bb in range(2):
                     r0 = P * (2 * pair + jl)
-                    nc.tensor.transpose(bank[:, jl, P * bb:P * (bb + 1)],
-                                        sT[:, 2 * which + bb, r0:r0 + P], ident[:])
-            st[("DU", g, pair, which)] = bank
+                    nc.tensor.transpose(bank[:, jl, P * bb:P * (bb + 1)], sT[:, bb, r0:r0 + P], ident[:])
+            st[("DU", n, which)] = bank
 
-        def stage_g(g, pair):
-            if pair == 0:
-                mt = res.tile([P, GT, MEM], F32, tag="m", name="mt")
-                st[("m", g)] = mt
-            mt = st[("m", g)]
+        def p1(n):
+            g, pair = n // 2, n % 2
             js = slice(2 * pair, 2 * pair + 2)
-            q = work.tile([P, 2, MEM], F32, tag="q", name="q")
-            t = work.tile([P, 2, MEM], F32, tag="t", name="t")
-            nc.vector.scalar_tensor_tensor(out=q[:], in0=st[("DU", g, pair, 0)][:], scalar=RHO,
+            q = res.tile([P, 2, MEM], F32, tag="q", name="q")
+            nc.vector.scalar_tensor_tensor(out=q[:], in0=st[("DU", n, 0)][:], scalar=RHO,
                                            in1=c_of[g][0][:, js, 0:MEM], op0=ALU.add, op1=ALU.mult)
+            st[("q", n)] = q
+
+        def p2(n):
+            g, pair = n // 2, n % 2
+            js = slice(2 * pair, 2 * pair + 2)
+            t = res.tile([P, 2, MEM], F32, tag="t", name="t")
             nc.vector.scalar_tensor_tensor(out=t[:], in0=hc_of[g][:, js, :], scalar=INV_BETA,
-                                           in1=q[:], op0=ALU.mult, op1=ALU.subtract)
-            nc.vector.tensor_tensor(out=t[:], in0=t[:], in1=st[("DU", g, pair, 1)][:], op=ALU.mult)
-            nc.vector.tensor_tensor(out=mt[:, js, :], in0=t[:], in1=q[:], op=ALU.add)
+                                           in1=st[("q", n)][:], op0=ALU.mult, op1=ALU.subtract)
+            st[("t", n)] = t
+
+        def p3(n):
+            t = st[("t", n)]
+            nc.vector.tensor_tensor(out=t[:], in0=t[:], in1=st[("DU", n, 1)][:], op=ALU.mult)
+
+        def p4(n):
+            g, pair = n // 2, n % 2
+            if pair == 0:
+                mt = res.tile([P, GT, MEM], F32, tag="m", name="mt", bufs=4)
+                st[("m", g)] = mt
+            js = slice(2 * pair, 2 * pair + 2)
+            nc.vector.tensor_tensor(out=st[("m", g)][:, js, :], in0=st[("t", n)][:], in1=st[("q", n)][:], op=ALU.add)
 
         def stage_h(g, pair):
             if pair == 0:
@@ -207,41 +224,64 @@ def tile_liquidmemorycell_pb_t_kernel(tc, x, h, h_candidate, Wd, bd, Wu, bu, out
             nc.gpsimd.tensor_tensor(out=rs[:], in0=rs[:], in1=st[("sh", g)][:], op=ALU.mult)
             st[("rs", g)] = rs
 
-        def stage_j(g):
-            o = res.tile([P, GT, MEM], F32, tag="o", name="o")
-            for jl in range(GT):
+        def stage_j(g, pair):
+            if pair == 0:
+                o = res.tile([P, GT, MEM], F32, tag="o", name="o")
+                st[("o", g)] = o
+            o = st[("o", g)]
+            for jl in range(2 * pair, 2 * pair + 2):
                 nc.vector.tensor_scalar(out=o[:, jl, :], in0=st[("m", g)][:, jl, :],
                                         scalar1=st[("rs", g)][:, jl:jl + 1], scalar2=None, op0=ALU.mult)
-            nc.sync.dma_start(out=ov[:, g * GT:(g + 1) * GT, :], in_=o[:])
+            if pair == 1:
+                nc.sync.dma_start(out=ov[:, g * GT:(g + 1) * GT, :], in_=o[:])
 
         def ok(g):
             return 0 <= g < NG
 
-        for it in range(-3, NG + 1):
+        def okp(n):
+            return 0 <= n < 2 * NG
+
+        for it in range(-3, NG + 2):
             if it == -2:
                 prep_weights()
             if ok(it + 3):
                 stage_a(it + 3)
+            if ok(it + 1):
+                stage_e(it + 1)
+            if okp(2 * it + 1):
+                p1(2 * it + 1)
+            if okp(2 * it + 2):
+                stage_f(2 * it + 2, 0)
+            if okp(2 * it):
+                p3(2 * it)
+            if okp(2 * it + 1):
+                stage_f(2 * it + 1, 1)
+                p2(2 * it + 1)
+            if okp(2 * it):
+                p4(2 * it)
             if ok(it - 1):
                 stage_h(it - 1, 1)
                 stage_i(it - 1)
-            if ok(it + 1):
-                stage_e(it + 1)
-            if ok(it):
-                stage_g(it, 0)
-                stage_f(it, 1, 0)
-                stage_f(it, 1, 1)
-                stage_h(it, 0)
             if ok(it + 2):
                 stage_c(it + 2)
                 stage_d(it + 2)
+            if ok(it - 2):
+                stage_j(it - 2, 0)
+            if okp(2 * it + 2):
+                p1(2 * it + 2)
+            if okp(2 * it + 3):
+                stage_f(2 * it + 3, 0)
+            if okp(2 * it + 1):
+                p3(2 * it + 1)
+            if okp(2 * it + 2):
+                stage_f(2 * it + 2, 1)
+                p2(2 * it + 2)
+            if okp(2 * it + 1):
+                p4(2 * it + 1)
             if ok(it):
-                stage_g(it, 1)
-            if ok(it + 1):
-                stage_f(it + 1, 0, 0)
-                stage_f(it + 1, 0, 1)
+                stage_h(it, 0)
             if ok(it + 3):
                 stage_k(it + 3)
                 stage_b(it + 3)
-            if ok(it - 1):
-                stage_j(it - 1)
+            if ok(it - 2):
+                stage_j(it - 2, 1)

@@ -21,6 +21,8 @@ NG = NT // GT
 FLOPS = 2 * B * DIN * 2 * MEM
 
 PIN = True
+B_ON_VECTOR_FROM = 2
+J_ON_GPSIMD_BELOW = NG - 2
 
 A_LOW = 0.1 + 1e-6
 SPAN = 10.0 - 0.1
@@ -66,27 +68,41 @@ def tile_liquidmemorycell_pb_t_kernel(tc, x, h, h_candidate, Wd, bd, Wu, bu, out
         c_of = {}
         hc_of = {}
         wraw = const.tile([P, 4, 2 * MEM], BF16, name="wraw")
+        chunk_tiles = []
         g0 = 0
         for ci, ng in enumerate(CHUNKS):
             nt = ng * GT
-            j0 = g0 * GT
             ctile = inp.tile([P, nt * DIN], BF16, name="c%d" % ci)
-            c3 = ctile[:].rearrange("p (j f) -> p j f", f=DIN)
-            nc.sync.dma_start(out=c3[:, :, 0:MEM], in_=hv[:, j0:j0 + nt, :])
-            nc.sync.dma_start(out=c3[:, :, MEM:DIN], in_=xv[:, j0:j0 + nt, :])
-            if ci == 0:
-                nc.sync.dma_start(out=wraw[:, :, 0:MEM], in_=Wd.rearrange("(p j) w -> p j w", j=4))
-                nc.sync.dma_start(out=wraw[:, :, MEM:2 * MEM], in_=Wu.rearrange("(p j) w -> p j w", j=4))
-                nc.sync.dma_start(out=brows[0:2, :], in_=bd.rearrange("(r c) -> r c", c=P))
-                nc.sync.dma_start(out=brows[2:4, :], in_=bu.rearrange("(r c) -> r c", c=P))
             hctile = inp.tile([P, nt * MEM], BF16, name="hc%d" % ci)
+            c3 = ctile[:].rearrange("p (j f) -> p j f", f=DIN)
             hc3 = hctile[:].rearrange("p (j f) -> p j f", f=MEM)
-            nc.sync.dma_start(out=hc3, in_=cv[:, j0:j0 + nt, :])
             cw = ctile[:].bitcast(F32).rearrange("p (j w u) -> p j u w", u=2, w=P)
+            chunk_tiles.append((c3, hc3, g0 * GT, nt))
             for k in range(ng):
                 c_of[g0 + k] = (c3[:, k * GT:(k + 1) * GT, :], cw[:, k * GT:(k + 1) * GT, :, :])
                 hc_of[g0 + k] = hc3[:, k * GT:(k + 1) * GT, :]
             g0 += ng
+
+        def load_c(ci):
+            c3, hc3, j0, nt = chunk_tiles[ci]
+            nc.sync.dma_start(out=c3[:, :, 0:MEM], in_=hv[:, j0:j0 + nt, :])
+            nc.sync.dma_start(out=c3[:, :, MEM:DIN], in_=xv[:, j0:j0 + nt, :])
+
+        def load_hc(ci):
+            c3, hc3, j0, nt = chunk_tiles[ci]
+            nc.sync.dma_start(out=hc3, in_=cv[:, j0:j0 + nt, :])
+
+        nc.sync.dma_start(out=wraw[:, :, 0:MEM], in_=Wd.rearrange("(p j) w -> p j w", j=4))
+        load_c(0)
+        nc.sync.dma_start(out=wraw[:, :, MEM:2 * MEM], in_=Wu.rearrange("(p j) w -> p j w", j=4))
+        nc.sync.dma_start(out=brows[0:2, :], in_=bd.rearrange("(r c) -> r c", c=P))
+        nc.sync.dma_start(out=brows[2:4, :], in_=bu.rearrange("(r c) -> r c", c=P))
+        load_c(1)
+        load_hc(0)
+        load_hc(1)
+        for ci in range(2, len(CHUNKS)):
+            load_c(ci)
+            load_hc(ci)
 
         if PIN:
             ctx.enter_context(tc.manual_schedule())
@@ -96,13 +112,19 @@ def tile_liquidmemorycell_pb_t_kernel(tc, x, h, h_candidate, Wd, bd, Wu, bu, out
         wcodes = const.tile([P, 2 * MEM], U32, name="wcodes", align_bytes=64)
         wscl = const.tile([P, 2 * MEM], U8, name="wscl", align_bytes=64)
 
-        def prep_weights():
-            wgrp = const.tile([P, 2 * MEM, 4], BF16, name="wgrp", align_bytes=64)
-            nc.vector.tensor_copy(out=wgrp[:], in_=wraw[:].rearrange("p j w -> p w j"))
-            ident_bf = const.tile([P, P], BF16, name="ident_bf")
-            nc.vector.tensor_copy(out=ident_bf[:], in_=ident[:])
-            nc.vector.quantize_mx(out=wcodes[:].bitcast(FP8X4), scales=wscl[:],
-                                  in_=wgrp[:].rearrange("p w j -> p (w j)"))
+        wgrp = const.tile([P, 2 * MEM, 4], BF16, name="wgrp", align_bytes=64)
+        ident_bf = const.tile([P, P], BF16, name="ident_bf")
+
+        def prep_regroup(which):
+            cols = slice(which * MEM, (which + 1) * MEM)
+            nc.vector.tensor_copy(out=wgrp[:, cols, :], in_=wraw[:, :, cols].rearrange("p j w -> p w j"))
+
+        def prep_quant(which):
+            cols = slice(which * MEM, (which + 1) * MEM)
+            nc.vector.quantize_mx(out=wcodes[:, cols].bitcast(FP8X4), scales=wscl[:, cols],
+                                  in_=wgrp[:, cols, :].rearrange("p w j -> p (w j)"))
+
+        def prep_bias():
             bps = psum.tile([P, P], BF16, tag="D", name="bps")
             nc.tensor.transpose(bps[:], brows[:], ident_bf[:])
             nc.vector.tensor_scalar(out=bias[:, 0:2], in0=bps[:, 0:2], scalar1=-1.0,
@@ -125,8 +147,12 @@ def tile_liquidmemorycell_pb_t_kernel(tc, x, h, h_candidate, Wd, bd, Wu, bu, out
             gw = grp[:].bitcast(F32).rearrange("p (r u) -> p r u", u=2)
             for half in range(2):
                 ct = st[("ct", g)][half]
-                nc.scalar.copy(out=gw[:, 2 * P * half:2 * P * (half + 1), :],
-                               in_=ct[:].rearrange("p u r -> p r u"))
+                if half == 1 and g >= B_ON_VECTOR_FROM:
+                    nc.vector.tensor_copy(out=gw[:, 2 * P * half:2 * P * (half + 1), :],
+                                          in_=ct[:].rearrange("p u r -> p r u"))
+                else:
+                    nc.scalar.copy(out=gw[:, 2 * P * half:2 * P * (half + 1), :],
+                                   in_=ct[:].rearrange("p u r -> p r u"))
             st[("grp", g)] = grp
 
         def stage_c(g):
@@ -221,7 +247,6 @@ def tile_liquidmemorycell_pb_t_kernel(tc, x, h, h_candidate, Wd, bd, Wu, bu, out
             rs = const.tile([P, GT], F32, name="rs%d" % g)
             nc.gpsimd.tensor_scalar_max(out=rs[:], in0=st[("ssm", g)][:], scalar1=CLAMP_M2)
             nc.gpsimd.tensor_tensor(out=rs[:], in0=rs[:], in1=neg_half[:], op=ALU.pow)
-            nc.gpsimd.tensor_tensor(out=rs[:], in0=rs[:], in1=st[("sh", g)][:], op=ALU.mult)
             st[("rs", g)] = rs
 
         def stage_j(g, pair):
@@ -230,8 +255,10 @@ def tile_liquidmemorycell_pb_t_kernel(tc, x, h, h_candidate, Wd, bd, Wu, bu, out
                 st[("o", g)] = o
             o = st[("o", g)]
             for jl in range(2 * pair, 2 * pair + 2):
-                nc.vector.tensor_scalar(out=o[:, jl, :], in0=st[("m", g)][:, jl, :],
-                                        scalar1=st[("rs", g)][:, jl:jl + 1], scalar2=None, op0=ALU.mult)
+                eng = nc.gpsimd if g < J_ON_GPSIMD_BELOW else nc.vector
+                eng.tensor_scalar(out=o[:, jl, :], in0=st[("m", g)][:, jl, :],
+                                  scalar1=st[("rs", g)][:, jl:jl + 1], scalar2=st[("sh", g)][:, jl:jl + 1],
+                                  op0=ALU.mult, op1=ALU.mult)
             if pair == 1:
                 nc.sync.dma_start(out=ov[:, g * GT:(g + 1) * GT, :], in_=o[:])
 
@@ -241,11 +268,15 @@ def tile_liquidmemorycell_pb_t_kernel(tc, x, h, h_candidate, Wd, bd, Wu, bu, out
         def okp(n):
             return 0 <= n < 2 * NG
 
+        nc.vector.tensor_copy(out=ident_bf[:], in_=ident[:])
+        prep_regroup(0)
         for it in range(-3, NG + 2):
-            if it == -2:
-                prep_weights()
-            if ok(it + 3):
-                stage_a(it + 3)
+            if it == -3:
+                stage_a(0)
+                prep_regroup(1)
+                prep_quant(0)
+                prep_quant(1)
+                prep_bias()
             if ok(it + 1):
                 stage_e(it + 1)
             if okp(2 * it + 1):
@@ -259,6 +290,8 @@ def tile_liquidmemorycell_pb_t_kernel(tc, x, h, h_candidate, Wd, bd, Wu, bu, out
                 p2(2 * it + 1)
             if okp(2 * it):
                 p4(2 * it)
+            if it > -3 and ok(it + 3):
+                stage_a(it + 3)
             if ok(it - 1):
                 stage_h(it - 1, 1)
                 stage_i(it - 1)
@@ -278,10 +311,11 @@ def tile_liquidmemorycell_pb_t_kernel(tc, x, h, h_candidate, Wd, bd, Wu, bu, out
                 p2(2 * it + 2)
             if okp(2 * it + 1):
                 p4(2 * it + 1)
+            if ok(it + 3):
+                stage_k(it + 3)
             if ok(it):
                 stage_h(it, 0)
             if ok(it + 3):
-                stage_k(it + 3)
                 stage_b(it + 3)
             if ok(it - 2):
                 stage_j(it - 2, 1)

@@ -22,7 +22,8 @@ FLOPS = 2 * B * DIN * 2 * MEM
 
 PIN = True
 B_ON_VECTOR_FROM = 2
-J_ON_GPSIMD_BELOW = NG - 2
+B_ON_VECTOR_EVERY = 3
+J_ON_GPSIMD_BELOW = 0
 
 A_LOW = 0.1 + 1e-6
 SPAN = 10.0 - 0.1
@@ -147,7 +148,7 @@ def tile_liquidmemorycell_pb_t_kernel(tc, x, h, h_candidate, Wd, bd, Wu, bu, out
             gw = grp[:].bitcast(F32).rearrange("p (r u) -> p r u", u=2)
             for half in range(2):
                 ct = st[("ct", g)][half]
-                if half == 1 and g >= B_ON_VECTOR_FROM:
+                if half == 1 and g >= B_ON_VECTOR_FROM and (g - B_ON_VECTOR_FROM) % B_ON_VECTOR_EVERY == 0:
                     nc.vector.tensor_copy(out=gw[:, 2 * P * half:2 * P * (half + 1), :],
                                           in_=ct[:].rearrange("p u r -> p r u"))
                 else:

@@ -18,12 +18,8 @@ DIN = MEM + IN_DIM
 NT = B // P
 GT = 4
 NG = NT // GT
+NP = 2 * NG
 FLOPS = 2 * B * DIN * 2 * MEM
-
-PIN = True
-B_ON_VECTOR_FROM = 2
-B_ON_VECTOR_EVERY = 3
-J_ON_GPSIMD_BELOW = 0
 
 A_LOW = 0.1 + 1e-6
 SPAN = 10.0 - 0.1
@@ -38,6 +34,10 @@ CLAMP_H2 = 1e-6 * 1e-6
 CHUNKS = [1, 1, 2, 2, 2, 2, 2, 2, 2]
 
 
+def copy_on_scalar(n):
+    return n % 4 == 1
+
+
 def tile_liquidmemorycell_pb_t_kernel(tc, x, h, h_candidate, Wd, bd, Wu, bu, out):
     nc = tc.nc
     assert sum(CHUNKS) == NG
@@ -45,7 +45,6 @@ def tile_liquidmemorycell_pb_t_kernel(tc, x, h, h_candidate, Wd, bd, Wu, bu, out
         const = ctx.enter_context(tc.tile_pool(name="const", bufs=1))
         inp = ctx.enter_context(tc.tile_pool(name="inp", bufs=1))
         work = ctx.enter_context(tc.tile_pool(name="work", bufs=2))
-        res = ctx.enter_context(tc.tile_pool(name="res", bufs=3))
         psum = ctx.enter_context(tc.psum_pool(name="psum", bufs=1))
 
         hv = h.rearrange("(p j) f -> p j f", j=NT)
@@ -59,8 +58,6 @@ def tile_liquidmemorycell_pb_t_kernel(tc, x, h, h_candidate, Wd, bd, Wu, bu, out
         nc.scalar.activation(out=warm2[:], in_=warm[:], func=ACT.Sigmoid)
         ident = const.tile([P, P], F32, name="ident")
         make_identity(nc, ident[:])
-        neg_half = const.tile([P, GT], F32, name="neg_half")
-        nc.gpsimd.memset(neg_half[:], -0.5)
         pos_half = const.tile([P, GT], F32, name="pos_half")
         nc.gpsimd.memset(pos_half[:], 0.5)
         brows = const.tile([P, P], BF16, name="brows")
@@ -79,9 +76,10 @@ def tile_liquidmemorycell_pb_t_kernel(tc, x, h, h_candidate, Wd, bd, Wu, bu, out
             hc3 = hctile[:].rearrange("p (j f) -> p j f", f=MEM)
             cw = ctile[:].bitcast(F32).rearrange("p (j w u) -> p j u w", u=2, w=P)
             chunk_tiles.append((c3, hc3, g0 * GT, nt))
-            for k in range(ng):
-                c_of[g0 + k] = (c3[:, k * GT:(k + 1) * GT, :], cw[:, k * GT:(k + 1) * GT, :, :])
-                hc_of[g0 + k] = hc3[:, k * GT:(k + 1) * GT, :]
+            for k in range(2 * ng):
+                js = slice(2 * k, 2 * k + 2)
+                c_of[2 * g0 + k] = (c3[:, js, :], cw[:, js, :, :])
+                hc_of[2 * g0 + k] = hc3[:, js, :]
             g0 += ng
 
         def load_c(ci):
@@ -105,14 +103,12 @@ def tile_liquidmemorycell_pb_t_kernel(tc, x, h, h_candidate, Wd, bd, Wu, bu, out
             load_c(ci)
             load_hc(ci)
 
-        if PIN:
-            ctx.enter_context(tc.manual_schedule())
+        ctx.enter_context(tc.manual_schedule())
 
         st = {}
         bias = const.tile([P, 4], F32, name="bias")
         wcodes = const.tile([P, 2 * MEM], U32, name="wcodes", align_bytes=64)
         wscl = const.tile([P, 2 * MEM], U8, name="wscl", align_bytes=64)
-
         wgrp = const.tile([P, 2 * MEM, 4], BF16, name="wgrp", align_bytes=64)
         ident_bf = const.tile([P, P], BF16, name="ident_bf")
 
@@ -126,35 +122,34 @@ def tile_liquidmemorycell_pb_t_kernel(tc, x, h, h_candidate, Wd, bd, Wu, bu, out
                                   in_=wgrp[:, cols, :].rearrange("p w j -> p (w j)"))
 
         def prep_bias():
-            bps = psum.tile([P, P], BF16, tag="D", name="bps")
+            bps = psum.tile([P, P], BF16, tag="P", name="bps")
             nc.tensor.transpose(bps[:], brows[:], ident_bf[:])
             nc.vector.tensor_scalar(out=bias[:, 0:2], in0=bps[:, 0:2], scalar1=-1.0,
                                     scalar2=-LN_KAPPA, op0=ALU.mult, op1=ALU.add)
             nc.vector.tensor_copy(out=bias[:, 2:4], in_=bps[:, 2:4])
 
-        def stage_a(g):
-            cw = c_of[g][1]
-            banks = []
-            for half in range(2):
-                ct = psum.tile([P, 2, 2 * P], F32, tag="ct%d" % half, name="ct")
-                for jl in range(2):
-                    for u in range(2):
-                        nc.tensor.transpose(ct[:, u, P * jl:P * (jl + 1)], cw[:, 2 * half + jl, u, :], ident[:])
-                banks.append(ct)
-            st[("ct", g)] = banks
+        def turn(dst, src, start=True, stop=True):
+            nc.tensor.matmul(dst, lhsT=src, rhs=ident[:], is_transpose=True, start=start, stop=stop)
 
-        def stage_b(g):
-            grp = work.tile([P, GT * P * 4], BF16, tag="grp", name="grp", align_bytes=64)
-            gw = grp[:].bitcast(F32).rearrange("p (r u) -> p r u", u=2)
-            for half in range(2):
-                ct = st[("ct", g)][half]
-                if half == 1 and g >= B_ON_VECTOR_FROM and (g - B_ON_VECTOR_FROM) % B_ON_VECTOR_EVERY == 0:
-                    nc.vector.tensor_copy(out=gw[:, 2 * P * half:2 * P * (half + 1), :],
-                                          in_=ct[:].rearrange("p u r -> p r u"))
-                else:
-                    nc.scalar.copy(out=gw[:, 2 * P * half:2 * P * (half + 1), :],
-                                   in_=ct[:].rearrange("p u r -> p r u"))
-            st[("grp", g)] = grp
+        def stage_a(n):
+            ct = psum.tile([P, 2, 2 * P], F32, tag="ct", name="ct", bufs=2)
+            for jl in range(2):
+                for u in range(2):
+                    turn(ct[:, u, P * jl:P * (jl + 1)], c_of[n][1][:, jl, u, :])
+            st[("ct", n)] = ct
+
+        def stage_b(n):
+            g, pair = n // 2, n % 2
+            if pair == 0:
+                grp = work.tile([P, GT * P * 4], BF16, tag="grp", name="grp", align_bytes=64)
+                st[("grp", g)] = grp
+            gw = st[("grp", g)][:].bitcast(F32).rearrange("p (r u) -> p r u", u=2)
+            dst = gw[:, 2 * P * pair:2 * P * (pair + 1), :]
+            src = st[("ct", n)][:].rearrange("p u r -> p r u")
+            if copy_on_scalar(n):
+                nc.scalar.copy(out=dst, in_=src)
+            else:
+                nc.vector.tensor_copy(out=dst, in_=src)
 
         def stage_c(g):
             codes = work.tile([P, GT * P], U32, tag="codes", name="codes", align_bytes=64)
@@ -162,161 +157,183 @@ def tile_liquidmemorycell_pb_t_kernel(tc, x, h, h_candidate, Wd, bd, Wu, bu, out
             nc.vector.quantize_mx(out=codes[:].bitcast(FP8X4), scales=scl[:], in_=st[("grp", g)][:])
             st[("codes", g)] = (codes, scl)
 
-        def stage_d(g):
+        def stage_x(n):
+            g, pair = n // 2, n % 2
             codes, scl = st[("codes", g)]
-            zs = []
-            for b in range(4):
-                z = psum.tile([P, GT * P], F32, tag="z%d" % b, name="z")
-                nc.tensor.matmul_mx(out=z[:], lhsT=wcodes[:, P * b:P * (b + 1)].bitcast(FP8X4),
-                                    lhsT_scale=wscl[:, P * b:P * (b + 1)],
-                                    rhs=codes[:].bitcast(FP8X4), rhs_scale=scl[:],
-                                    start=True, stop=True)
-                zs.append(z)
-            st[("z", g)] = zs
-
-        def stage_e(g):
-            halves = []
+            rows = slice(2 * P * pair, 2 * P * (pair + 1))
             for which in range(2):
-                sT = work.tile([P, 2, GT * P], F32, tag="sT%d" % which, name="sT")
+                z = psum.tile([P, 2, 2 * P], F32, tag="z%d" % which, name="z")
+                for bb in range(2):
+                    cols = slice(P * (2 * which + bb), P * (2 * which + bb + 1))
+                    nc.tensor.matmul_mx(out=z[:, bb, :], lhsT=wcodes[:, cols].bitcast(FP8X4),
+                                        lhsT_scale=wscl[:, cols],
+                                        rhs=codes[:, rows].bitcast(FP8X4), rhs_scale=scl[:, rows],
+                                        start=True, stop=True)
+                st[("z", n, which)] = z
+
+        def stage_e(n):
+            for which in range(2):
+                sT = work.tile([P, 2, 2 * P], F32, tag="sT%d" % which, name="sT", bufs=4)
                 for bb in range(2):
                     b = 2 * which + bb
-                    nc.scalar.activation(out=sT[:, bb, :], in_=st[("z", g)][b][:], func=ACT.Sigmoid,
+                    nc.scalar.activation(out=sT[:, bb, :], in_=st[("z", n, which)][:, bb, :], func=ACT.Sigmoid,
                                          bias=bias[:, b:b + 1], scale=(-1.0 if which == 0 else 1.0))
-                halves.append(sT)
-            st[("sT", g)] = halves
+                st[("sT", n, which)] = sT
 
-        def stage_f(n, which):
-            g, pair = n // 2, n % 2
-            sT = st[("sT", g)][which]
-            bank = psum.tile([P, 2, MEM], F32, tag=("D" if which == 0 else "U"), name="bank")
+        def stage_hc(n):
+            cn = work.tile([P, 2, MEM], F32, tag="cn", name="cn", bufs=4)
+            nc.gpsimd.tensor_scalar(out=cn[:], in0=hc_of[n], scalar1=-INV_BETA, scalar2=0.0,
+                                    op0=ALU.mult, op1=ALU.add)
+            st[("cn", n)] = cn
+
+        def stage_f(n):
+            bank = psum.tile([P, 2, MEM], F32, tag="D", name="bank")
             for jl in range(2):
                 for bb in range(2):
-                    r0 = P * (2 * pair + jl)
-                    nc.tensor.transpose(bank[:, jl, P * bb:P * (bb + 1)], sT[:, bb, r0:r0 + P], ident[:])
-            st[("DU", n, which)] = bank
+                    turn(bank[:, jl, P * bb:P * (bb + 1)], st[("sT", n, 0)][:, bb, P * jl:P * (jl + 1)])
+            st[("D", n)] = bank
 
-        def p1(n):
-            g, pair = n // 2, n % 2
-            js = slice(2 * pair, 2 * pair + 2)
-            q = res.tile([P, 2, MEM], F32, tag="q", name="q")
-            nc.vector.scalar_tensor_tensor(out=q[:], in0=st[("DU", n, 0)][:], scalar=RHO,
-                                           in1=c_of[g][0][:, js, 0:MEM], op0=ALU.add, op1=ALU.mult)
+        def v1(n):
+            q = work.tile([P, 2, MEM], F32, tag="q", name="q", bufs=5)
+            nc.vector.scalar_tensor_tensor(out=q[:], in0=st[("D", n)][:], scalar=RHO,
+                                           in1=c_of[n][0][:, :, 0:MEM], op0=ALU.add, op1=ALU.mult)
             st[("q", n)] = q
 
-        def p2(n):
-            g, pair = n // 2, n % 2
-            js = slice(2 * pair, 2 * pair + 2)
-            t = res.tile([P, 2, MEM], F32, tag="t", name="t")
-            nc.vector.scalar_tensor_tensor(out=t[:], in0=hc_of[g][:, js, :], scalar=INV_BETA,
-                                           in1=st[("q", n)][:], op0=ALU.mult, op1=ALU.subtract)
-            st[("t", n)] = t
+        def stage_g(n):
+            bank = psum.tile([P, 2, 2 * P], F32, tag="T", name="bank")
+            for jl in range(2):
+                for bb in range(2):
+                    dst = bank[:, bb, P * jl:P * (jl + 1)]
+                    turn(dst, st[("q", n)][:, jl, P * bb:P * (bb + 1)], True, False)
+                    turn(dst, st[("cn", n)][:, jl, P * bb:P * (bb + 1)], False, True)
+            st[("T", n)] = bank
 
-        def p3(n):
-            t = st[("t", n)]
-            nc.vector.tensor_tensor(out=t[:], in0=t[:], in1=st[("DU", n, 1)][:], op=ALU.mult)
+        def v2(n):
+            pT = work.tile([P, 2, 2 * P], F32, tag="pT", name="pT", bufs=3)
+            nc.vector.tensor_tensor(out=pT[:], in0=st[("T", n)][:], in1=st[("sT", n, 1)][:], op=ALU.mult)
+            st[("pT", n)] = pT
 
-        def p4(n):
+        def stage_h(n):
+            bank = psum.tile([P, 2, MEM], F32, tag="P", name="bank")
+            for jl in range(2):
+                for bb in range(2):
+                    turn(bank[:, jl, P * bb:P * (bb + 1)], st[("pT", n)][:, bb, P * jl:P * (jl + 1)])
+            st[("P", n)] = bank
+
+        def v3(n):
             g, pair = n // 2, n % 2
             if pair == 0:
-                mt = res.tile([P, GT, MEM], F32, tag="m", name="mt", bufs=4)
+                mt = work.tile([P, GT, MEM], F32, tag="m", name="mt", bufs=4)
                 st[("m", g)] = mt
             js = slice(2 * pair, 2 * pair + 2)
-            nc.vector.tensor_tensor(out=st[("m", g)][:, js, :], in0=st[("t", n)][:], in1=st[("q", n)][:], op=ALU.add)
+            nc.vector.tensor_tensor(out=st[("m", g)][:, js, :], in0=st[("q", n)][:], in1=st[("P", n)][:],
+                                    op=ALU.subtract)
 
-        def stage_h(g, pair):
+        def square_sum(src, dst):
+            junk = work.tile([P, MEM], BF16, tag="junk", name="junk")
+            nc.scalar.activation(out=junk[:], in_=src, func=ACT.Square, accum_out=dst)
+
+        def stage_k(n):
+            g, pair = n // 2, n % 2
+            if pair == 0:
+                ssh = const.tile([P, GT], F32, name="ssh%d" % g)
+                st[("ssh", g)] = ssh
+            for jl in range(2):
+                col = 2 * pair + jl
+                square_sum(c_of[n][0][:, jl, 0:MEM], st[("ssh", g)][:, col:col + 1])
+
+        def stage_sq(n):
+            g, pair = n // 2, n % 2
             if pair == 0:
                 ssm = const.tile([P, GT], F32, name="ssm%d" % g)
                 st[("ssm", g)] = ssm
-            ssm = st[("ssm", g)]
-            for jl in range(2 * pair, 2 * pair + 2):
-                junk = work.tile([P, MEM], BF16, tag="junk", name="junk")
-                nc.scalar.activation(out=junk[:], in_=st[("m", g)][:, jl, :], func=ACT.Square,
-                                     accum_out=ssm[:, jl:jl + 1])
+            for jl in range(2):
+                col = 2 * pair + jl
+                square_sum(st[("m", g)][:, col, :], st[("ssm", g)][:, col:col + 1])
 
-        def stage_k(g):
-            ssh = const.tile([P, GT], F32, name="ssh%d" % g)
-            for jl in range(GT):
-                junk = work.tile([P, MEM], BF16, tag="junk", name="junk")
-                nc.scalar.activation(out=junk[:], in_=c_of[g][0][:, jl, 0:MEM], func=ACT.Square,
-                                     accum_out=ssh[:, jl:jl + 1])
-            sh = const.tile([P, GT], F32, name="sh%d" % g)
-            nc.gpsimd.tensor_scalar_max(out=sh[:], in0=ssh[:], scalar1=CLAMP_H2)
-            nc.gpsimd.tensor_tensor(out=sh[:], in0=sh[:], in1=pos_half[:], op=ALU.pow)
-            st[("sh", g)] = sh
+        def stat1(g):
+            sm = const.tile([P, GT], F32, name="sm%d" % g)
+            nc.vector.tensor_scalar_max(out=sm[:], in0=st[("ssm", g)][:], scalar1=CLAMP_M2)
+            st[("sm", g)] = sm
 
-        def stage_i(g):
-            rs = const.tile([P, GT], F32, name="rs%d" % g)
-            nc.gpsimd.tensor_scalar_max(out=rs[:], in0=st[("ssm", g)][:], scalar1=CLAMP_M2)
-            nc.gpsimd.tensor_tensor(out=rs[:], in0=rs[:], in1=neg_half[:], op=ALU.pow)
-            st[("rs", g)] = rs
+        def stat2(g):
+            rc = const.tile([P, GT], F32, name="rc%d" % g)
+            nc.vector.reciprocal(out=rc[:], in_=st[("sm", g)][:])
+            st[("rc", g)] = rc
 
-        def stage_j(g, pair):
+        def stat3(g):
+            ra = const.tile([P, GT], F32, name="ra%d" % g)
+            nc.vector.scalar_tensor_tensor(out=ra[:], in0=st[("ssh", g)][:], scalar=CLAMP_H2,
+                                           in1=st[("rc", g)][:], op0=ALU.max, op1=ALU.mult)
+            st[("ra", g)] = ra
+
+        def stat4(g):
+            rt = const.tile([P, GT], F32, name="rt%d" % g)
+            nc.gpsimd.tensor_tensor(out=rt[:], in0=st[("ra", g)][:], in1=pos_half[:], op=ALU.pow)
+            st[("rt", g)] = rt
+
+        def stage_j(n):
+            g, pair = n // 2, n % 2
             if pair == 0:
-                o = res.tile([P, GT, MEM], F32, tag="o", name="o")
+                o = work.tile([P, GT, MEM], F32, tag="o", name="o", bufs=3)
                 st[("o", g)] = o
             o = st[("o", g)]
             for jl in range(2 * pair, 2 * pair + 2):
-                eng = nc.gpsimd if g < J_ON_GPSIMD_BELOW else nc.vector
-                eng.tensor_scalar(out=o[:, jl, :], in0=st[("m", g)][:, jl, :],
-                                  scalar1=st[("rs", g)][:, jl:jl + 1], scalar2=st[("sh", g)][:, jl:jl + 1],
-                                  op0=ALU.mult, op1=ALU.mult)
+                nc.gpsimd.tensor_scalar(out=o[:, jl, :], in0=st[("m", g)][:, jl, :],
+                                        scalar1=st[("rt", g)][:, jl:jl + 1], scalar2=0.0,
+                                        op0=ALU.mult, op1=ALU.add)
             if pair == 1:
                 nc.sync.dma_start(out=ov[:, g * GT:(g + 1) * GT, :], in_=o[:])
 
-        def ok(g):
-            return 0 <= g < NG
-
-        def okp(n):
-            return 0 <= n < 2 * NG
+        def ok(n):
+            return 0 <= n < NP
 
         nc.vector.tensor_copy(out=ident_bf[:], in_=ident[:])
         prep_regroup(0)
-        for it in range(-3, NG + 2):
-            if it == -3:
-                stage_a(0)
+        for i in range(-6, NP + 7):
+            odd = i % 2 == 1
+            if ok(i - 3):
+                v3(i - 3)
+            if ok(i - 1):
+                stage_g(i - 1)
+            if ok(i):
+                stage_f(i)
+            if ok(i - 2):
+                stage_h(i - 2)
+            if odd and ok(i - 5):
+                stat1((i - 5) // 2)
+            if ok(i + 1):
+                stage_e(i + 1)
+            if ok(i + 5) and not copy_on_scalar(i + 5):
+                stage_b(i + 5)
+            if i == -5:
                 prep_regroup(1)
                 prep_quant(0)
-                prep_quant(1)
                 prep_bias()
-            if ok(it + 1):
-                stage_e(it + 1)
-            if okp(2 * it + 1):
-                p1(2 * it + 1)
-            if okp(2 * it + 2):
-                stage_f(2 * it + 2, 0)
-            if okp(2 * it):
-                p3(2 * it)
-            if okp(2 * it + 1):
-                stage_f(2 * it + 1, 1)
-                p2(2 * it + 1)
-            if okp(2 * it):
-                p4(2 * it)
-            if it > -3 and ok(it + 3):
-                stage_a(it + 3)
-            if ok(it - 1):
-                stage_h(it - 1, 1)
-                stage_i(it - 1)
-            if ok(it + 2):
-                stage_c(it + 2)
-                stage_d(it + 2)
-            if ok(it - 2):
-                stage_j(it - 2, 0)
-            if okp(2 * it + 2):
-                p1(2 * it + 2)
-            if okp(2 * it + 3):
-                stage_f(2 * it + 3, 0)
-            if okp(2 * it + 1):
-                p3(2 * it + 1)
-            if okp(2 * it + 2):
-                stage_f(2 * it + 2, 1)
-                p2(2 * it + 2)
-            if okp(2 * it + 1):
-                p4(2 * it + 1)
-            if ok(it + 3):
-                stage_k(it + 3)
-            if ok(it):
-                stage_h(it, 0)
-            if ok(it + 3):
-                stage_b(it + 3)
-            if ok(it - 2):
-                stage_j(it - 2, 1)
+            if odd and ok(i + 3):
+                stage_c((i + 3) // 2)
+            if i == -3:
+                prep_quant(1)
+            if odd and ok(i - 5):
+                stat2((i - 5) // 2)
+            if ok(i - 1):
+                v2(i - 1)
+            if odd and ok(i - 5):
+                stat3((i - 5) // 2)
+                stat4((i - 5) // 2)
+            if ok(i):
+                v1(i)
+            if ok(i + 6):
+                stage_a(i + 6)
+            if ok(i + 2):
+                stage_x(i + 2)
+            if ok(i + 4):
+                stage_k(i + 4)
+            if ok(i + 5) and copy_on_scalar(i + 5):
+                stage_b(i + 5)
+            if ok(i - 3):
+                stage_sq(i - 3)
+            if ok(i + 2):
+                stage_hc(i + 2)
+            if ok(i - 6):
+                stage_j(i - 6)

@@ -19,6 +19,7 @@ NT = B // P
 GT = 4
 NG = NT // GT
 NP = 2 * NG
+HALF = MEM // 2
 FLOPS = 2 * B * DIN * 2 * MEM
 
 A_LOW = 0.1 + 1e-6
@@ -31,7 +32,9 @@ INV_BETA = 1.0 / BETA
 CLAMP_M2 = (1e-12 / BETA) * (1e-12 / BETA)
 CLAMP_H2 = 1e-6 * 1e-6
 
-CHUNKS = [1, 1, 2, 2, 2, 2, 2, 2, 2]
+CHUNKS = [1, 1, 2, 4, 4, 4, 4, 4, 4, 4]
+UNITS = [(n, 2) for n in range(0, NP - 2, 2)] + [(NP - 2, 1), (NP - 1, 1)]
+J_ON_VECTOR_FROM = NP - 6
 
 
 def copy_on_scalar(n):
@@ -40,7 +43,7 @@ def copy_on_scalar(n):
 
 def tile_liquidmemorycell_pb_t_kernel(tc, x, h, h_candidate, Wd, bd, Wu, bu, out):
     nc = tc.nc
-    assert sum(CHUNKS) == NG
+    assert sum(CHUNKS) == NP
     with ExitStack() as ctx:
         const = ctx.enter_context(tc.tile_pool(name="const", bufs=1))
         inp = ctx.enter_context(tc.tile_pool(name="inp", bufs=1))
@@ -65,47 +68,58 @@ def tile_liquidmemorycell_pb_t_kernel(tc, x, h, h_candidate, Wd, bd, Wu, bu, out
 
         c_of = {}
         hc_of = {}
-        wraw = const.tile([P, 4, 2 * MEM], BF16, name="wraw")
+        wraw = [const.tile([P, 4, MEM], BF16, name="wraw%d" % which) for which in range(2)]
         chunk_tiles = []
         g0 = 0
         for ci, ng in enumerate(CHUNKS):
-            nt = ng * GT
+            nt = ng * 2
             ctile = inp.tile([P, nt * DIN], BF16, name="c%d" % ci)
             hctile = inp.tile([P, nt * MEM], BF16, name="hc%d" % ci)
-            c3 = ctile[:].rearrange("p (j f) -> p j f", f=DIN)
             hc3 = hctile[:].rearrange("p (j f) -> p j f", f=MEM)
-            cw = ctile[:].bitcast(F32).rearrange("p (j w u) -> p j u w", u=2, w=P)
-            chunk_tiles.append((c3, hc3, g0 * GT, nt))
-            for k in range(2 * ng):
+            c5 = ctile[:].rearrange("p (j u a f) -> p j u a f", u=2, a=2, f=HALF)
+            cw = ctile[:].bitcast(F32).rearrange("p (j u w) -> p j u w", u=2, w=P)
+            chunk_tiles.append((c5, hc3, 2 * g0, nt))
+            for k in range(ng):
                 js = slice(2 * k, 2 * k + 2)
-                c_of[2 * g0 + k] = (c3[:, js, :], cw[:, js, :, :])
-                hc_of[2 * g0 + k] = hc3[:, js, :]
+                c_of[g0 + k] = (c5[:, js, :, 0, :], cw[:, js, :, :])
+                hc_of[g0 + k] = hc3[:, js, :]
             g0 += ng
 
         def load_c(ci):
-            c3, hc3, j0, nt = chunk_tiles[ci]
-            nc.sync.dma_start(out=c3[:, :, 0:MEM], in_=hv[:, j0:j0 + nt, :])
-            nc.sync.dma_start(out=c3[:, :, MEM:DIN], in_=xv[:, j0:j0 + nt, :])
+            c5, hc3, j0, nt = chunk_tiles[ci]
+            for s, src in enumerate((hv, xv)):
+                nc.sync.dma_start(out=c5[:, :, :, s, :],
+                                  in_=src[:, j0:j0 + nt, :].rearrange("p j (u f) -> p j u f", u=2))
 
         def load_hc(ci):
-            c3, hc3, j0, nt = chunk_tiles[ci]
+            c5, hc3, j0, nt = chunk_tiles[ci]
             nc.sync.dma_start(out=hc3, in_=cv[:, j0:j0 + nt, :])
 
-        nc.sync.dma_start(out=wraw[:, :, 0:MEM], in_=Wd.rearrange("(p j) w -> p j w", j=4))
+        def load_w(which, src):
+            for s in range(2):
+                half = slice(P // 2 * s, P // 2 * (s + 1))
+                nc.sync.dma_start(out=wraw[which][half, :, :].rearrange("p (u e) w -> p u (e w)", u=2),
+                                  in_=src[MEM * s:MEM * (s + 1), :].rearrange("(u p e) w -> p u (e w)", u=2, e=2))
+
         load_c(0)
-        nc.sync.dma_start(out=wraw[:, :, MEM:2 * MEM], in_=Wu.rearrange("(p j) w -> p j w", j=4))
+        load_w(0, Wd)
+        load_w(1, Wu)
+        load_c(1)
         nc.sync.dma_start(out=brows[0:2, :], in_=bd.rearrange("(r c) -> r c", c=P))
         nc.sync.dma_start(out=brows[2:4, :], in_=bu.rearrange("(r c) -> r c", c=P))
-        load_c(1)
         load_hc(0)
+        load_c(2)
         load_hc(1)
-        for ci in range(2, len(CHUNKS)):
+        load_hc(2)
+        for ci in range(3, len(CHUNKS)):
             load_c(ci)
             load_hc(ci)
 
         ctx.enter_context(tc.manual_schedule())
 
         st = {}
+        unit_of = {n: u for u in UNITS for n in range(u[0], u[0] + u[1])}
+        unit_ending = {u[0] + u[1] - 1: u for u in UNITS}
         bias = const.tile([P, 4], F32, name="bias")
         wcodes = const.tile([P, 2 * MEM], U32, name="wcodes", align_bytes=64)
         wscl = const.tile([P, 2 * MEM], U8, name="wscl", align_bytes=64)
@@ -114,7 +128,7 @@ def tile_liquidmemorycell_pb_t_kernel(tc, x, h, h_candidate, Wd, bd, Wu, bu, out
 
         def prep_regroup(which):
             cols = slice(which * MEM, (which + 1) * MEM)
-            nc.vector.tensor_copy(out=wgrp[:, cols, :], in_=wraw[:, :, cols].rearrange("p j w -> p w j"))
+            nc.vector.tensor_copy(out=wgrp[:, cols, :], in_=wraw[which][:].rearrange("p j w -> p w j"))
 
         def prep_quant(which):
             cols = slice(which * MEM, (which + 1) * MEM)
@@ -132,48 +146,43 @@ def tile_liquidmemorycell_pb_t_kernel(tc, x, h, h_candidate, Wd, bd, Wu, bu, out
             nc.tensor.matmul(dst, lhsT=src, rhs=ident[:], is_transpose=True, start=start, stop=stop)
 
         def stage_a(n):
-            ct = psum.tile([P, 2, 2 * P], F32, tag="ct", name="ct", bufs=2)
+            ct = psum.tile([P, 2, 2 * P], F32, tag="ct", name="ct")
             for jl in range(2):
                 for u in range(2):
                     turn(ct[:, u, P * jl:P * (jl + 1)], c_of[n][1][:, jl, u, :])
             st[("ct", n)] = ct
 
         def stage_b(n):
-            g, pair = n // 2, n % 2
-            if pair == 0:
-                grp = work.tile([P, GT * P * 4], BF16, tag="grp", name="grp", align_bytes=64)
-                st[("grp", g)] = grp
-            gw = st[("grp", g)][:].bitcast(F32).rearrange("p (r u) -> p r u", u=2)
-            dst = gw[:, 2 * P * pair:2 * P * (pair + 1), :]
+            grp = work.tile([P, 2 * P * 4], BF16, tag="grp", name="grp", align_bytes=64)
+            st[("grp", n)] = grp
+            dst = grp[:].bitcast(F32).rearrange("p (r u) -> p r u", u=2)
             src = st[("ct", n)][:].rearrange("p u r -> p r u")
             if copy_on_scalar(n):
                 nc.scalar.copy(out=dst, in_=src)
             else:
                 nc.vector.tensor_copy(out=dst, in_=src)
 
-        def stage_c(g):
-            codes = work.tile([P, GT * P], U32, tag="codes", name="codes", align_bytes=64)
-            scl = work.tile([P, GT * P], U8, tag="scl", name="scl", align_bytes=64)
-            nc.vector.quantize_mx(out=codes[:].bitcast(FP8X4), scales=scl[:], in_=st[("grp", g)][:])
-            st[("codes", g)] = (codes, scl)
+        def stage_c(n):
+            codes = work.tile([P, 2 * P], U32, tag="codes", name="codes", align_bytes=64)
+            scl = work.tile([P, 2 * P], U8, tag="scl", name="scl", align_bytes=64)
+            nc.vector.quantize_mx(out=codes[:].bitcast(FP8X4), scales=scl[:], in_=st[("grp", n)][:])
+            st[("codes", n)] = (codes, scl)
 
         def stage_x(n):
-            g, pair = n // 2, n % 2
-            codes, scl = st[("codes", g)]
-            rows = slice(2 * P * pair, 2 * P * (pair + 1))
+            codes, scl = st[("codes", n)]
             for which in range(2):
-                z = psum.tile([P, 2, 2 * P], F32, tag="z%d" % which, name="z")
+                z = psum.tile([P, 2, 2 * P], F32, tag="z", name="z", bufs=3)
                 for bb in range(2):
                     cols = slice(P * (2 * which + bb), P * (2 * which + bb + 1))
                     nc.tensor.matmul_mx(out=z[:, bb, :], lhsT=wcodes[:, cols].bitcast(FP8X4),
                                         lhsT_scale=wscl[:, cols],
-                                        rhs=codes[:, rows].bitcast(FP8X4), rhs_scale=scl[:, rows],
+                                        rhs=codes[:].bitcast(FP8X4), rhs_scale=scl[:],
                                         start=True, stop=True)
                 st[("z", n, which)] = z
 
         def stage_e(n):
             for which in range(2):
-                sT = work.tile([P, 2, 2 * P], F32, tag="sT%d" % which, name="sT", bufs=4)
+                sT = work.tile([P, 2, 2 * P], F32, tag="sT%d" % which, name="sT", bufs=5)
                 for bb in range(2):
                     b = 2 * which + bb
                     nc.scalar.activation(out=sT[:, bb, :], in_=st[("z", n, which)][:, bb, :], func=ACT.Sigmoid,
@@ -194,13 +203,14 @@ def tile_liquidmemorycell_pb_t_kernel(tc, x, h, h_candidate, Wd, bd, Wu, bu, out
             st[("D", n)] = bank
 
         def v1(n):
-            q = work.tile([P, 2, MEM], F32, tag="q", name="q", bufs=5)
-            nc.vector.scalar_tensor_tensor(out=q[:], in0=st[("D", n)][:], scalar=RHO,
-                                           in1=c_of[n][0][:, :, 0:MEM], op0=ALU.add, op1=ALU.mult)
+            q = work.tile([P, 2, MEM], F32, tag="q", name="q", bufs=6)
+            nc.vector.scalar_tensor_tensor(out=q[:].rearrange("p j (u f) -> p j u f", u=2),
+                                           in0=st[("D", n)][:].rearrange("p j (u f) -> p j u f", u=2), scalar=RHO,
+                                           in1=c_of[n][0], op0=ALU.add, op1=ALU.mult)
             st[("q", n)] = q
 
         def stage_g(n):
-            bank = psum.tile([P, 2, 2 * P], F32, tag="T", name="bank")
+            bank = psum.tile([P, 2, 2 * P], F32, tag="T", name="bank", bufs=2)
             for jl in range(2):
                 for bb in range(2):
                     dst = bank[:, bb, P * jl:P * (jl + 1)]
@@ -221,119 +231,119 @@ def tile_liquidmemorycell_pb_t_kernel(tc, x, h, h_candidate, Wd, bd, Wu, bu, out
             st[("P", n)] = bank
 
         def v3(n):
-            g, pair = n // 2, n % 2
-            if pair == 0:
-                mt = work.tile([P, GT, MEM], F32, tag="m", name="mt", bufs=4)
-                st[("m", g)] = mt
-            js = slice(2 * pair, 2 * pair + 2)
-            nc.vector.tensor_tensor(out=st[("m", g)][:, js, :], in0=st[("q", n)][:], in1=st[("P", n)][:],
-                                    op=ALU.subtract)
+            mt = work.tile([P, 2, MEM], F32, tag="m", name="mt", bufs=6)
+            nc.vector.tensor_tensor(out=mt[:], in0=st[("q", n)][:], in1=st[("P", n)][:], op=ALU.subtract)
+            st[("m", n)] = mt
 
         def square_sum(src, dst):
-            junk = work.tile([P, MEM], BF16, tag="junk", name="junk")
+            junk = work.tile([P, 2, HALF], BF16, tag="junk", name="junk")
             nc.scalar.activation(out=junk[:], in_=src, func=ACT.Square, accum_out=dst)
 
+        def sums(kind, n):
+            first, count = unit_of[n]
+            if n == first:
+                ss = const.tile([P, 2 * count], F32, name="%s%d" % (kind, first))
+                st[(kind, first)] = ss
+            return st[(kind, first)], 2 * (n - first)
+
         def stage_k(n):
-            g, pair = n // 2, n % 2
-            if pair == 0:
-                ssh = const.tile([P, GT], F32, name="ssh%d" % g)
-                st[("ssh", g)] = ssh
+            ssh, col = sums("ssh", n)
             for jl in range(2):
-                col = 2 * pair + jl
-                square_sum(c_of[n][0][:, jl, 0:MEM], st[("ssh", g)][:, col:col + 1])
+                square_sum(c_of[n][0][:, jl, :, :], ssh[:, col + jl:col + jl + 1])
 
         def stage_sq(n):
-            g, pair = n // 2, n % 2
-            if pair == 0:
-                ssm = const.tile([P, GT], F32, name="ssm%d" % g)
-                st[("ssm", g)] = ssm
+            ssm, col = sums("ssm", n)
             for jl in range(2):
-                col = 2 * pair + jl
-                square_sum(st[("m", g)][:, col, :], st[("ssm", g)][:, col:col + 1])
+                square_sum(st[("m", n)][:, jl, :].rearrange("p (u f) -> p u f", u=2), ssm[:, col + jl:col + jl + 1])
 
-        def stat1(g):
-            sm = const.tile([P, GT], F32, name="sm%d" % g)
-            nc.vector.tensor_scalar_max(out=sm[:], in0=st[("ssm", g)][:], scalar1=CLAMP_M2)
-            st[("sm", g)] = sm
+        def stat(kind, first, count):
+            s = const.tile([P, 2 * count], F32, name="%s%d" % (kind, first))
+            st[(kind, first)] = s
+            return s
 
-        def stat2(g):
-            rc = const.tile([P, GT], F32, name="rc%d" % g)
-            nc.vector.reciprocal(out=rc[:], in_=st[("sm", g)][:])
-            st[("rc", g)] = rc
+        def stat1(first, count):
+            sm = stat("sm", first, count)
+            nc.vector.tensor_scalar_max(out=sm[:], in0=st[("ssm", first)][:], scalar1=CLAMP_M2)
 
-        def stat3(g):
-            ra = const.tile([P, GT], F32, name="ra%d" % g)
-            nc.vector.scalar_tensor_tensor(out=ra[:], in0=st[("ssh", g)][:], scalar=CLAMP_H2,
-                                           in1=st[("rc", g)][:], op0=ALU.max, op1=ALU.mult)
-            st[("ra", g)] = ra
+        def stat2(first, count):
+            rc = stat("rc", first, count)
+            nc.vector.reciprocal(out=rc[:], in_=st[("sm", first)][:])
 
-        def stat4(g):
-            rt = const.tile([P, GT], F32, name="rt%d" % g)
-            nc.gpsimd.tensor_tensor(out=rt[:], in0=st[("ra", g)][:], in1=pos_half[:], op=ALU.pow)
-            st[("rt", g)] = rt
+        def stat3(first, count):
+            ra = stat("ra", first, count)
+            nc.vector.scalar_tensor_tensor(out=ra[:], in0=st[("ssh", first)][:], scalar=CLAMP_H2,
+                                           in1=st[("rc", first)][:], op0=ALU.max, op1=ALU.mult)
+
+        def stat4(first, count):
+            rt = stat("rt", first, count)
+            nc.gpsimd.tensor_tensor(out=rt[:], in0=st[("ra", first)][:], in1=pos_half[:, 0:2 * count], op=ALU.pow)
 
         def stage_j(n):
-            g, pair = n // 2, n % 2
-            if pair == 0:
-                o = work.tile([P, GT, MEM], F32, tag="o", name="o", bufs=3)
-                st[("o", g)] = o
-            o = st[("o", g)]
-            for jl in range(2 * pair, 2 * pair + 2):
-                nc.gpsimd.tensor_scalar(out=o[:, jl, :], in0=st[("m", g)][:, jl, :],
-                                        scalar1=st[("rt", g)][:, jl:jl + 1], scalar2=0.0,
-                                        op0=ALU.mult, op1=ALU.add)
-            if pair == 1:
-                nc.sync.dma_start(out=ov[:, g * GT:(g + 1) * GT, :], in_=o[:])
+            first, count = unit_of[n]
+            if n == first:
+                o = work.tile([P, 2 * count, MEM], F32, tag="o%d" % count, name="o", bufs=3)
+                st[("o", first)] = o
+            o = st[("o", first)]
+            eng = nc.vector if n >= J_ON_VECTOR_FROM else nc.gpsimd
+            for jl in range(2):
+                col = 2 * (n - first) + jl
+                eng.tensor_scalar(out=o[:, col, :], in0=st[("m", n)][:, jl, :],
+                                  scalar1=st[("rt", first)][:, col:col + 1], scalar2=0.0,
+                                  op0=ALU.mult, op1=ALU.add)
+            if n == first + count - 1:
+                nc.sync.dma_start(out=ov[:, 2 * first:2 * (n + 1), :], in_=o[:])
 
         def ok(n):
             return 0 <= n < NP
 
         nc.vector.tensor_copy(out=ident_bf[:], in_=ident[:])
-        prep_regroup(0)
-        for i in range(-6, NP + 7):
-            odd = i % 2 == 1
-            if ok(i - 3):
-                v3(i - 3)
-            if ok(i - 1):
-                stage_g(i - 1)
+        for i in range(-3, NP + 10):
+            unit = unit_ending.get(i - 6)
+            if ok(i - 4):
+                v3(i - 4)
             if ok(i):
                 stage_f(i)
-            if ok(i - 2):
-                stage_h(i - 2)
-            if odd and ok(i - 5):
-                stat1((i - 5) // 2)
             if ok(i + 1):
-                stage_e(i + 1)
-            if ok(i + 5) and not copy_on_scalar(i + 5):
-                stage_b(i + 5)
-            if i == -5:
-                prep_regroup(1)
-                prep_quant(0)
-                prep_bias()
-            if odd and ok(i + 3):
-                stage_c((i + 3) // 2)
-            if i == -3:
-                prep_quant(1)
-            if odd and ok(i - 5):
-                stat2((i - 5) // 2)
+                stage_x(i + 1)
+            if ok(i - 3):
+                stage_h(i - 3)
             if ok(i - 1):
-                v2(i - 1)
-            if odd and ok(i - 5):
-                stat3((i - 5) // 2)
-                stat4((i - 5) // 2)
+                stage_g(i - 1)
+            if unit:
+                stat1(*unit)
+            if ok(i + 2):
+                stage_b(i + 2)
+            if i == -2:
+                prep_regroup(0)
+            if unit:
+                stat2(*unit)
+            if ok(i - 2):
+                v2(i - 2)
+            if unit:
+                stat3(*unit)
             if ok(i):
                 v1(i)
-            if ok(i + 6):
-                stage_a(i + 6)
+            if ok(i + 3):
+                stage_a(i + 3)
+            if i == -2:
+                prep_bias()
             if ok(i + 2):
-                stage_x(i + 2)
-            if ok(i + 4):
-                stage_k(i + 4)
-            if ok(i + 5) and copy_on_scalar(i + 5):
-                stage_b(i + 5)
-            if ok(i - 3):
-                stage_sq(i - 3)
-            if ok(i + 2):
-                stage_hc(i + 2)
-            if ok(i - 6):
-                stage_j(i - 6)
+                stage_c(i + 2)
+            if i == -2:
+                prep_quant(0)
+                prep_regroup(1)
+                prep_quant(1)
+            if ok(i + 1):
+                stage_e(i + 1)
+            if ok(i + 3):
+                stage_k(i + 3)
+            if ok(i - 4):
+                stage_sq(i - 4)
+            if ok(i + 1):
+                stage_hc(i + 1)
+            if ok(i - 8) and i - 8 < J_ON_VECTOR_FROM:
+                stage_j(i - 8)
+            if ok(i - 9) and i - 9 >= J_ON_VECTOR_FROM:
+                stage_j(i - 9)
+            if unit:
+                stat4(*unit)

@@ -32,7 +32,8 @@ INV_BETA = 1.0 / BETA
 CLAMP_M2 = (1e-12 / BETA) * (1e-12 / BETA)
 CLAMP_H2 = 1e-6 * 1e-6
 
-CHUNKS = [1, 1, 2, 4, 4, 4, 4, 4, 4, 4]
+CHUNKS = [1, 1, 1, 1] + [2] * 14
+FIRST_LOADS = 7
 UNITS = [(n, 2) for n in range(0, NP - 2, 2)] + [(NP - 2, 1), (NP - 1, 1)]
 J_ON_VECTOR_FROM = NP - 6
 
@@ -103,16 +104,14 @@ def tile_liquidmemorycell_pb_t_kernel(tc, x, h, h_candidate, Wd, bd, Wu, bu, out
 
         load_c(0)
         load_w(0, Wd)
-        load_w(1, Wu)
-        load_c(1)
         nc.sync.dma_start(out=brows[0:2, :], in_=bd.rearrange("(r c) -> r c", c=P))
         nc.sync.dma_start(out=brows[2:4, :], in_=bu.rearrange("(r c) -> r c", c=P))
-        load_hc(0)
-        load_c(2)
-        load_hc(1)
-        load_hc(2)
-        for ci in range(3, len(CHUNKS)):
+        load_c(1)
+        load_w(1, Wu)
+        for ci in range(2, FIRST_LOADS):
             load_c(ci)
+            load_hc(ci - 2)
+        for ci in range(FIRST_LOADS - 2, FIRST_LOADS):
             load_hc(ci)
 
         ctx.enter_context(tc.manual_schedule())
@@ -168,17 +167,16 @@ def tile_liquidmemorycell_pb_t_kernel(tc, x, h, h_candidate, Wd, bd, Wu, bu, out
             nc.vector.quantize_mx(out=codes[:].bitcast(FP8X4), scales=scl[:], in_=st[("grp", n)][:])
             st[("codes", n)] = (codes, scl)
 
-        def stage_x(n):
+        def stage_x(n, which):
             codes, scl = st[("codes", n)]
-            for which in range(2):
-                z = psum.tile([P, 2, 2 * P], F32, tag="z", name="z", bufs=3)
-                for bb in range(2):
-                    cols = slice(P * (2 * which + bb), P * (2 * which + bb + 1))
-                    nc.tensor.matmul_mx(out=z[:, bb, :], lhsT=wcodes[:, cols].bitcast(FP8X4),
-                                        lhsT_scale=wscl[:, cols],
-                                        rhs=codes[:].bitcast(FP8X4), rhs_scale=scl[:],
-                                        start=True, stop=True)
-                st[("z", n, which)] = z
+            z = psum.tile([P, 2, 2 * P], F32, tag="z", name="z", bufs=3)
+            for bb in range(2):
+                cols = slice(P * (2 * which + bb), P * (2 * which + bb + 1))
+                nc.tensor.matmul_mx(out=z[:, bb, :], lhsT=wcodes[:, cols].bitcast(FP8X4),
+                                    lhsT_scale=wscl[:, cols],
+                                    rhs=codes[:].bitcast(FP8X4), rhs_scale=scl[:],
+                                    start=True, stop=True)
+            st[("z", n, which)] = z
 
         def stage_e(n):
             for which in range(2):
@@ -281,7 +279,7 @@ def tile_liquidmemorycell_pb_t_kernel(tc, x, h, h_candidate, Wd, bd, Wu, bu, out
         def stage_j(n):
             first, count = unit_of[n]
             if n == first:
-                o = work.tile([P, 2 * count, MEM], F32, tag="o%d" % count, name="o", bufs=3)
+                o = work.tile([P, 2 * count, MEM], F32, tag="o%d" % count, name="o", bufs=4)
                 st[("o", first)] = o
             o = st[("o", first)]
             eng = nc.vector if n >= J_ON_VECTOR_FROM else nc.gpsimd
@@ -299,12 +297,17 @@ def tile_liquidmemorycell_pb_t_kernel(tc, x, h, h_candidate, Wd, bd, Wu, bu, out
         nc.vector.tensor_copy(out=ident_bf[:], in_=ident[:])
         for i in range(-3, NP + 10):
             unit = unit_ending.get(i - 6)
+            if i >= 0 and i % 2 == 0 and FIRST_LOADS + i // 2 < len(CHUNKS):
+                load_c(FIRST_LOADS + i // 2)
+                load_hc(FIRST_LOADS + i // 2)
             if ok(i - 4):
                 v3(i - 4)
             if ok(i):
                 stage_f(i)
             if ok(i + 1):
-                stage_x(i + 1)
+                stage_x(i + 1, 0)
+            if ok(i + 1) and i >= 0:
+                stage_x(i + 1, 1)
             if ok(i - 3):
                 stage_h(i - 3)
             if ok(i - 1):
@@ -325,14 +328,15 @@ def tile_liquidmemorycell_pb_t_kernel(tc, x, h, h_candidate, Wd, bd, Wu, bu, out
                 v1(i)
             if ok(i + 3):
                 stage_a(i + 3)
-            if i == -2:
-                prep_bias()
             if ok(i + 2):
                 stage_c(i + 2)
             if i == -2:
                 prep_quant(0)
+                prep_bias()
                 prep_regroup(1)
+            if i == -1:
                 prep_quant(1)
+                stage_x(0, 1)
             if ok(i + 1):
                 stage_e(i + 1)
             if ok(i + 3):

@@ -35,11 +35,14 @@ CLAMP_H2 = 1e-6 * 1e-6
 CHUNKS = [1, 1, 1, 1] + [2] * 14
 FIRST_LOADS = 7
 UNITS = [(n, 2) for n in range(0, NP - 2, 2)] + [(NP - 2, 1), (NP - 1, 1)]
-J_ON_VECTOR_FROM = NP - 6
 
 
 def copy_on_scalar(n):
-    return n % 4 == 1
+    return n % 2 == 1
+
+
+def scale_on_vector(n):
+    return n % 4 < 2 or n >= NP - 6
 
 
 def tile_liquidmemorycell_pb_t_kernel(tc, x, h, h_candidate, Wd, bd, Wu, bu, out):
@@ -222,7 +225,7 @@ def tile_liquidmemorycell_pb_t_kernel(tc, x, h, h_candidate, Wd, bd, Wu, bu, out
             st[("pT", n)] = pT
 
         def stage_h(n):
-            bank = psum.tile([P, 2, MEM], F32, tag="P", name="bank")
+            bank = psum.tile([P, 2, MEM], F32, tag=("ct" if n >= NP - 4 and n % 2 else "P"), name="bank")
             for jl in range(2):
                 for bb in range(2):
                     turn(bank[:, jl, P * bb:P * (bb + 1)], st[("pT", n)][:, bb, P * jl:P * (jl + 1)])
@@ -282,7 +285,7 @@ def tile_liquidmemorycell_pb_t_kernel(tc, x, h, h_candidate, Wd, bd, Wu, bu, out
                 o = work.tile([P, 2 * count, MEM], F32, tag="o%d" % count, name="o", bufs=4)
                 st[("o", first)] = o
             o = st[("o", first)]
-            eng = nc.vector if n >= J_ON_VECTOR_FROM else nc.gpsimd
+            eng = nc.vector if scale_on_vector(n) else nc.gpsimd
             for jl in range(2):
                 col = 2 * (n - first) + jl
                 eng.tensor_scalar(out=o[:, col, :], in0=st[("m", n)][:, jl, :],
@@ -326,8 +329,6 @@ def tile_liquidmemorycell_pb_t_kernel(tc, x, h, h_candidate, Wd, bd, Wu, bu, out
                 stat3(*unit)
             if ok(i):
                 v1(i)
-            if ok(i + 3):
-                stage_a(i + 3)
             if ok(i + 2):
                 stage_c(i + 2)
             if i == -2:
@@ -337,6 +338,8 @@ def tile_liquidmemorycell_pb_t_kernel(tc, x, h, h_candidate, Wd, bd, Wu, bu, out
             if i == -1:
                 prep_quant(1)
                 stage_x(0, 1)
+            if ok(i + 3):
+                stage_a(i + 3)
             if ok(i + 1):
                 stage_e(i + 1)
             if ok(i + 3):
@@ -345,9 +348,9 @@ def tile_liquidmemorycell_pb_t_kernel(tc, x, h, h_candidate, Wd, bd, Wu, bu, out
                 stage_sq(i - 4)
             if ok(i + 1):
                 stage_hc(i + 1)
-            if ok(i - 8) and i - 8 < J_ON_VECTOR_FROM:
+            if ok(i - 8) and not scale_on_vector(i - 8):
                 stage_j(i - 8)
-            if ok(i - 9) and i - 9 >= J_ON_VECTOR_FROM:
+            if ok(i - 9) and scale_on_vector(i - 9):
                 stage_j(i - 9)
             if unit:
                 stat4(*unit)

@@ -41,8 +41,12 @@ def copy_on_scalar(n):
     return n % 2 == 1
 
 
+def in_rows(n):
+    return n % 4 == 3
+
+
 def scale_on_vector(n):
-    return n % 4 < 2 or n >= NP - 6
+    return n >= NP - 6
 
 
 def tile_liquidmemorycell_pb_t_kernel(tc, x, h, h_candidate, Wd, bd, Wu, bu, out):
@@ -210,18 +214,28 @@ def tile_liquidmemorycell_pb_t_kernel(tc, x, h, h_candidate, Wd, bd, Wu, bu, out
                                            in1=c_of[n][0], op0=ALU.add, op1=ALU.mult)
             st[("q", n)] = q
 
+        def p2(n):
+            t = work.tile([P, 2, MEM], F32, tag="t", name="t", bufs=3)
+            nc.vector.scalar_tensor_tensor(out=t[:], in0=hc_of[n], scalar=INV_BETA, in1=st[("q", n)][:],
+                                           op0=ALU.mult, op1=ALU.subtract)
+            st[("t", n)] = t
+
         def stage_g(n):
             bank = psum.tile([P, 2, 2 * P], F32, tag="T", name="bank", bufs=2)
             for jl in range(2):
                 for bb in range(2):
                     dst = bank[:, bb, P * jl:P * (jl + 1)]
-                    turn(dst, st[("q", n)][:, jl, P * bb:P * (bb + 1)], True, False)
-                    turn(dst, st[("cn", n)][:, jl, P * bb:P * (bb + 1)], False, True)
+                    if in_rows(n):
+                        turn(bank[:, jl, P * bb:P * (bb + 1)], st[("sT", n, 1)][:, bb, P * jl:P * (jl + 1)])
+                    else:
+                        turn(dst, st[("q", n)][:, jl, P * bb:P * (bb + 1)], True, False)
+                        turn(dst, st[("cn", n)][:, jl, P * bb:P * (bb + 1)], False, True)
             st[("T", n)] = bank
 
         def v2(n):
             pT = work.tile([P, 2, 2 * P], F32, tag="pT", name="pT", bufs=3)
-            nc.vector.tensor_tensor(out=pT[:], in0=st[("T", n)][:], in1=st[("sT", n, 1)][:], op=ALU.mult)
+            other = st[("t", n)] if in_rows(n) else st[("sT", n, 1)]
+            nc.vector.tensor_tensor(out=pT[:], in0=st[("T", n)][:], in1=other[:], op=ALU.mult)
             st[("pT", n)] = pT
 
         def stage_h(n):
@@ -233,7 +247,10 @@ def tile_liquidmemorycell_pb_t_kernel(tc, x, h, h_candidate, Wd, bd, Wu, bu, out
 
         def v3(n):
             mt = work.tile([P, 2, MEM], F32, tag="m", name="mt", bufs=6)
-            nc.vector.tensor_tensor(out=mt[:], in0=st[("q", n)][:], in1=st[("P", n)][:], op=ALU.subtract)
+            if in_rows(n):
+                nc.vector.tensor_tensor(out=mt[:], in0=st[("q", n)][:], in1=st[("pT", n)][:], op=ALU.add)
+            else:
+                nc.vector.tensor_tensor(out=mt[:], in0=st[("q", n)][:], in1=st[("P", n)][:], op=ALU.subtract)
             st[("m", n)] = mt
 
         def square_sum(src, dst):
@@ -311,7 +328,7 @@ def tile_liquidmemorycell_pb_t_kernel(tc, x, h, h_candidate, Wd, bd, Wu, bu, out
                 stage_x(i + 1, 0)
             if ok(i + 1) and i >= 0:
                 stage_x(i + 1, 1)
-            if ok(i - 3):
+            if ok(i - 3) and not in_rows(i - 3):
                 stage_h(i - 3)
             if ok(i - 1):
                 stage_g(i - 1)
@@ -331,6 +348,8 @@ def tile_liquidmemorycell_pb_t_kernel(tc, x, h, h_candidate, Wd, bd, Wu, bu, out
                 v1(i)
             if ok(i + 2):
                 stage_c(i + 2)
+            if ok(i) and in_rows(i):
+                p2(i)
             if i == -2:
                 prep_quant(0)
                 prep_bias()
@@ -346,7 +365,7 @@ def tile_liquidmemorycell_pb_t_kernel(tc, x, h, h_candidate, Wd, bd, Wu, bu, out
                 stage_k(i + 3)
             if ok(i - 4):
                 stage_sq(i - 4)
-            if ok(i + 1):
+            if ok(i + 1) and not in_rows(i + 1):
                 stage_hc(i + 1)
             if ok(i - 8) and not scale_on_vector(i - 8):
                 stage_j(i - 8)

@@ -185,14 +185,13 @@ def tile_liquidmemorycell_pb_t_kernel(tc, x, h, h_candidate, Wd, bd, Wu, bu, out
                                     start=True, stop=True)
             st[("z", n, which)] = z
 
-        def stage_e(n):
-            for which in range(2):
-                sT = work.tile([P, 2, 2 * P], F32, tag="sT%d" % which, name="sT", bufs=5)
-                for bb in range(2):
-                    b = 2 * which + bb
-                    nc.scalar.activation(out=sT[:, bb, :], in_=st[("z", n, which)][:, bb, :], func=ACT.Sigmoid,
-                                         bias=bias[:, b:b + 1], scale=(-1.0 if which == 0 else 1.0))
-                st[("sT", n, which)] = sT
+        def stage_e(n, which):
+            sT = work.tile([P, 2, 2 * P], F32, tag="sT%d" % which, name="sT", bufs=5)
+            for bb in range(2):
+                b = 2 * which + bb
+                nc.scalar.activation(out=sT[:, bb, :], in_=st[("z", n, which)][:, bb, :], func=ACT.Sigmoid,
+                                     bias=bias[:, b:b + 1], scale=(-1.0 if which == 0 else 1.0))
+            st[("sT", n, which)] = sT
 
         def stage_hc(n):
             cn = work.tile([P, 2, MEM], F32, tag="cn", name="cn", bufs=4)
@@ -322,7 +321,7 @@ def tile_liquidmemorycell_pb_t_kernel(tc, x, h, h_candidate, Wd, bd, Wu, bu, out
                 load_hc(FIRST_LOADS + i // 2)
             if ok(i - 4):
                 v3(i - 4)
-            if ok(i):
+            if ok(i) and i > 0:
                 stage_f(i)
             if ok(i + 1):
                 stage_x(i + 1, 0)
@@ -334,18 +333,20 @@ def tile_liquidmemorycell_pb_t_kernel(tc, x, h, h_candidate, Wd, bd, Wu, bu, out
                 stage_g(i - 1)
             if unit:
                 stat1(*unit)
+            if i == 0:
+                v1(0)
             if ok(i + 2):
                 stage_b(i + 2)
             if i == -2:
                 prep_regroup(0)
-            if unit:
-                stat2(*unit)
             if ok(i - 2):
                 v2(i - 2)
             if unit:
-                stat3(*unit)
-            if ok(i):
+                stat2(*unit)
+            if ok(i) and i > 0:
                 v1(i)
+            if unit:
+                stat3(*unit)
             if ok(i + 2):
                 stage_c(i + 2)
             if ok(i) and in_rows(i):
@@ -356,11 +357,15 @@ def tile_liquidmemorycell_pb_t_kernel(tc, x, h, h_candidate, Wd, bd, Wu, bu, out
                 prep_regroup(1)
             if i == -1:
                 prep_quant(1)
+                stage_e(0, 0)
+                stage_f(0)
                 stage_x(0, 1)
             if ok(i + 3):
                 stage_a(i + 3)
+            if ok(i + 1) and i >= 0:
+                stage_e(i + 1, 0)
             if ok(i + 1):
-                stage_e(i + 1)
+                stage_e(i + 1, 1)
             if ok(i + 3):
                 stage_k(i + 3)
             if ok(i - 4):

import math
from contextlib import ExitStack

import concourse.mybir as mybir
from concourse.masks import make_identity

F32 = mybir.dt.float32
BF16 = mybir.dt.bfloat16
U32 = mybir.dt.uint32
U8 = mybir.dt.uint8
FP8X4 = mybir.dt.float8_e4m3fn_x4
ALU = mybir.AluOpType
ACT = mybir.ActivationFunctionType

P = 128
B, IN_DIM, MEM = 8192, 256, 256
DIN = MEM + IN_DIM
NT = B // P
GT = 4
NG = NT // GT
NP = 2 * NG
HALF = MEM // 2
FLOPS = 2 * B * DIN * 2 * MEM

A_LOW = 0.1 + 1e-6
SPAN = 10.0 - 0.1
KAPPA = (A_LOW + SPAN) / A_LOW
LN_KAPPA = math.log(KAPPA)
BETA = SPAN / (A_LOW * (A_LOW + SPAN))
RHO = A_LOW / SPAN
INV_BETA = 1.0 / BETA
CLAMP_M2 = (1e-12 / BETA) * (1e-12 / BETA)
CLAMP_H2 = 1e-6 * 1e-6

CHUNKS = [1, 1, 1, 1] + [2] * 14
FIRST_LOADS = 7
UNITS = [(n, 2) for n in range(0, NP - 2, 2)] + [(NP - 2, 1), (NP - 1, 1)]


def copy_on_scalar(n):
    return n % 2 == 1


def in_rows(n):
    return n % 4 == 3


def scale_on_vector(n):
    return n >= NP - 6


def tile_liquidmemorycell_pb_t_kernel(tc, x, h, h_candidate, Wd, bd, Wu, bu, out):
    nc = tc.nc
    assert sum(CHUNKS) == NP
    with ExitStack() as ctx:
        const = ctx.enter_context(tc.tile_pool(name="const", bufs=1))
        inp = ctx.enter_context(tc.tile_pool(name="inp", bufs=1))
        work = ctx.enter_context(tc.tile_pool(name="work", bufs=2))
        psum = ctx.enter_context(tc.psum_pool(name="psum", bufs=1))

        hv = h.rearrange("(p j) f -> p j f", j=NT)
        xv = x.rearrange("(p j) f -> p j f", j=NT)
        cv = h_candidate.rearrange("(p j) f -> p j f", j=NT)
        ov = out.rearrange("(p j) f -> p j f", j=NT)

        warm = const.tile([P, 1], F32, name="warm")
        nc.vector.memset(warm[:], 0.0)
        warm2 = const.tile([P, 1], F32, name="warm2")
        nc.scalar.activation(out=warm2[:], in_=warm[:], func=ACT.Sigmoid)
        ident = const.tile([P, P], F32, name="ident")
        make_identity(nc, ident[:])
        pos_half = const.tile([P, GT], F32, name="pos_half")
        nc.gpsimd.memset(pos_half[:], 0.5)
        brows = const.tile([P, P], BF16, name="brows")
        nc.gpsimd.memset(brows[:], 0.0)

        c_of = {}
        hc_of = {}
        wraw = [const.tile([P, 4, MEM], BF16, name="wraw%d" % which) for which in range(2)]
        chunk_tiles = []
        g0 = 0
        for ci, ng in enumerate(CHUNKS):
            nt = ng * 2
            ctile = inp.tile([P, nt * DIN], BF16, name="c%d" % ci)
            hctile = inp.tile([P, nt * MEM], BF16, name="hc%d" % ci)
            hc3 = hctile[:].rearrange("p (j f) -> p j f", f=MEM)
            c5 = ctile[:].rearrange("p (j u a f) -> p j u a f", u=2, a=2, f=HALF)
            cw = ctile[:].bitcast(F32).rearrange("p (j u w) -> p j u w", u=2, w=P)
            chunk_tiles.append((c5, hc3, 2 * g0, nt))
            for k in range(ng):
                js = slice(2 * k, 2 * k + 2)
                c_of[g0 + k] = (c5[:, js, :, 0, :], cw[:, js, :, :])
                hc_of[g0 + k] = hc3[:, js, :]
            g0 += ng

        def load_c(ci):
            c5, hc3, j0, nt = chunk_tiles[ci]
            for s, src in enumerate((hv, xv)):
                nc.sync.dma_start(out=c5[:, :, :, s, :],
                                  in_=src[:, j0:j0 + nt, :].rearrange("p j (u f) -> p j u f", u=2))

        def load_hc(ci):
            c5, hc3, j0, nt = chunk_tiles[ci]
            nc.sync.dma_start(out=hc3, in_=cv[:, j0:j0 + nt, :])

        def load_w(which, src):
            for s in range(2):
                half = slice(P // 2 * s, P // 2 * (s + 1))
                nc.sync.dma_start(out=wraw[which][half, :, :].rearrange("p (u e) w -> p u (e w)", u=2),
                                  in_=src[MEM * s:MEM * (s + 1), :].rearrange("(u p e) w -> p u (e w)", u=2, e=2))

        load_c(0)
        load_w(0, Wd)
        nc.sync.dma_start(out=brows[0:2, :], in_=bd.rearrange("(r c) -> r c", c=P))
        nc.sync.dma_start(out=brows[2:4, :], in_=bu.rearrange("(r c) -> r c", c=P))
        load_c(1)
        load_w(1, Wu)
        for ci in range(2, FIRST_LOADS):
            load_c(ci)
            load_hc(ci - 2)
        for ci in range(FIRST_LOADS - 2, FIRST_LOADS):
            load_hc(ci)

        ctx.enter_context(tc.manual_schedule())

        st = {}
        unit_of = {n: u for u in UNITS for n in range(u[0], u[0] + u[1])}
        unit_ending = {u[0] + u[1] - 1: u for u in UNITS}
        bias = const.tile([P, 4], F32, name="bias")
        wcodes = const.tile([P, 2 * MEM], U32, name="wcodes", align_bytes=64)
        wscl = const.tile([P, 2 * MEM], U8, name="wscl", align_bytes=64)
        wgrp = const.tile([P, 2 * MEM, 4], BF16, name="wgrp", align_bytes=64)
        ident_bf = const.tile([P, P], BF16, name="ident_bf")

        def prep_regroup(which):
            cols = slice(which * MEM, (which + 1) * MEM)
            nc.vector.tensor_copy(out=wgrp[:, cols, :], in_=wraw[which][:].rearrange("p j w -> p w j"))

        def prep_quant(which):
            cols = slice(which * MEM, (which + 1) * MEM)
            nc.vector.quantize_mx(out=wcodes[:, cols].bitcast(FP8X4), scales=wscl[:, cols],
                                  in_=wgrp[:, cols, :].rearrange("p w j -> p (w j)"))

        def prep_bias():
            bps = psum.tile([P, P], BF16, tag="P", name="bps")
            nc.tensor.transpose(bps[:], brows[:], ident_bf[:])
            nc.vector.tensor_scalar(out=bias[:, 0:2], in0=bps[:, 0:2], scalar1=-1.0,
                                    scalar2=-LN_KAPPA, op0=ALU.mult, op1=ALU.add)
            nc.vector.tensor_copy(out=bias[:, 2:4], in_=bps[:, 2:4])

        def turn(dst, src, start=True, stop=True):
            nc.tensor.matmul(dst, lhsT=src, rhs=ident[:], is_transpose=True, start=start, stop=stop)

        def stage_a(n):
            ct = psum.tile([P, 2, 2 * P], F32, tag="ct", name="ct")
            for jl in range(2):
                for u in range(2):
                    turn(ct[:, u, P * jl:P * (jl + 1)], c_of[n][1][:, jl, u, :])
            st[("ct", n)] = ct

        def stage_b(n):
            grp = work.tile([P, 2 * P * 4], BF16, tag="grp", name="grp", align_bytes=64)
            st[("grp", n)] = grp
            dst = grp[:].bitcast(F32).rearrange("p (r u) -> p r u", u=2)
            src = st[("ct", n)][:].rearrange("p u r -> p r u")
            if copy_on_scalar(n):
                nc.scalar.copy(out=dst, in_=src)
            else:
                nc.vector.tensor_copy(out=dst, in_=src)

        def stage_c(n):
            codes = work.tile([P, 2 * P], U32, tag="codes", name="codes", align_bytes=64)
            scl = work.tile([P, 2 * P], U8, tag="scl", name="scl", align_bytes=64)
            nc.vector.quantize_mx(out=codes[:].bitcast(FP8X4), scales=scl[:], in_=st[("grp", n)][:])
            st[("codes", n)] = (codes, scl)

        def stage_x(n, which):
            codes, scl = st[("codes", n)]
            z = psum.tile([P, 2, 2 * P], F32, tag="z", name="z", bufs=3)
            for bb in range(2):
                cols = slice(P * (2 * which + bb), P * (2 * which + bb + 1))
                nc.tensor.matmul_mx(out=z[:, bb, :], lhsT=wcodes[:, cols].bitcast(FP8X4),
                                    lhsT_scale=wscl[:, cols],
                                    rhs=codes[:].bitcast(FP8X4), rhs_scale=scl[:],
                                    start=True, stop=True)
            st[("z", n, which)] = z

        def stage_e(n, which):
            sT = work.tile([P, 2, 2 * P], F32, tag="sT%d" % which, name="sT", bufs=5)
            for bb in range(2):
                b = 2 * which + bb
                nc.scalar.activation(out=sT[:, bb, :], in_=st[("z", n, which)][:, bb, :], func=ACT.Sigmoid,
                                     bias=bias[:, b:b + 1], scale=(-1.0 if which == 0 else 1.0))
            st[("sT", n, which)] = sT

        def stage_hc(n):
            cn = work.tile([P, 2, MEM], F32, tag="cn", name="cn", bufs=4)
            nc.gpsimd.tensor_scalar(out=cn[:], in0=hc_of[n], scalar1=-INV_BETA, scalar2=0.0,
                                    op0=ALU.mult, op1=ALU.add)
            st[("cn", n)] = cn

        def stage_f(n):
            bank = psum.tile([P, 2, MEM], F32, tag="D", name="bank")
            for jl in range(2):
                for bb in range(2):
                    turn(bank[:, jl, P * bb:P * (bb + 1)], st[("sT", n, 0)][:, bb, P * jl:P * (jl + 1)])
            st[("D", n)] = bank

        def v1(n):
            q = work.tile([P, 2, MEM], F32, tag="q", name="q", bufs=6)
            nc.vector.scalar_tensor_tensor(out=q[:].rearrange("p j (u f) -> p j u f", u=2),
                                           in0=st[("D", n)][:].rearrange("p j (u f) -> p j u f", u=2), scalar=RHO,
                                           in1=c_of[n][0], op0=ALU.add, op1=ALU.mult)
            st[("q", n)] = q

        def p2(n):
            t = work.tile([P, 2, MEM], F32, tag="t", name="t", bufs=3)
            nc.vector.scalar_tensor_tensor(out=t[:], in0=hc_of[n], scalar=INV_BETA, in1=st[("q", n)][:],
                                           op0=ALU.mult, op1=ALU.subtract)
            st[("t", n)] = t

        def stage_g(n):
            bank = psum.tile([P, 2, 2 * P], F32, tag="T", name="bank", bufs=2)
            for jl in range(2):
                for bb in range(2):
                    dst = bank[:, bb, P * jl:P * (jl + 1)]
                    if in_rows(n):
                        turn(bank[:, jl, P * bb:P * (bb + 1)], st[("sT", n, 1)][:, bb, P * jl:P * (jl + 1)])
                    else:
                        turn(dst, st[("q", n)][:, jl, P * bb:P * (bb + 1)], True, False)
                        turn(dst, st[("cn", n)][:, jl, P * bb:P * (bb + 1)], False, True)
            st[("T", n)] = bank

        def v2(n):
            pT = work.tile([P, 2, 2 * P], F32, tag="pT", name="pT", bufs=3)
            other = st[("t", n)] if in_rows(n) else st[("sT", n, 1)]
            nc.vector.tensor_tensor(out=pT[:], in0=st[("T", n)][:], in1=other[:], op=ALU.mult)
            st[("pT", n)] = pT

        def stage_h(n):
            bank = psum.tile([P, 2, MEM], F32, tag=("ct" if n >= NP - 4 and n % 2 else "P"), name="bank")
            for jl in range(2):
                for bb in range(2):
                    turn(bank[:, jl, P * bb:P * (bb + 1)], st[("pT", n)][:, bb, P * jl:P * (jl + 1)])
            st[("P", n)] = bank

        def v3(n):
            mt = work.tile([P, 2, MEM], F32, tag="m", name="mt", bufs=6)
            if in_rows(n):
                nc.vector.tensor_tensor(out=mt[:], in0=st[("q", n)][:], in1=st[("pT", n)][:], op=ALU.add)
            else:
                nc.vector.tensor_tensor(out=mt[:], in0=st[("q", n)][:], in1=st[("P", n)][:], op=ALU.subtract)
            st[("m", n)] = mt

        def square_sum(src, dst):
            junk = work.tile([P, 2, HALF], BF16, tag="junk", name="junk")
            nc.scalar.activation(out=junk[:], in_=src, func=ACT.Square, accum_out=dst)

        def sums(kind, n):
            first, count = unit_of[n]
            if n == first:
                ss = const.tile([P, 2 * count], F32, name="%s%d" % (kind, first))
                st[(kind, first)] = ss
            return st[(kind, first)], 2 * (n - first)

        def stage_k(n):
            ssh, col = sums("ssh", n)
            for jl in range(2):
                square_sum(c_of[n][0][:, jl, :, :], ssh[:, col + jl:col + jl + 1])

        def stage_sq(n):
            ssm, col = sums("ssm", n)
            for jl in range(2):
                square_sum(st[("m", n)][:, jl, :].rearrange("p (u f) -> p u f", u=2), ssm[:, col + jl:col + jl + 1])

        def stat(kind, first, count):
            s = const.tile([P, 2 * count], F32, name="%s%d" % (kind, first))
            st[(kind, first)] = s
            return s

        def stat1(first, count):
            sm = stat("sm", first, count)
            nc.vector.tensor_scalar_max(out=sm[:], in0=st[("ssm", first)][:], scalar1=CLAMP_M2)

        def stat2(first, count):
            rc = stat("rc", first, count)
            nc.vector.reciprocal(out=rc[:], in_=st[("sm", first)][:])

        def stat3(first, count):
            ra = stat("ra", first, count)
            nc.vector.scalar_tensor_tensor(out=ra[:], in0=st[("ssh", first)][:], scalar=CLAMP_H2,
                                           in1=st[("rc", first)][:], op0=ALU.max, op1=ALU.mult)

        def stat4(first, count):
            rt = stat("rt", first, count)
            nc.gpsimd.tensor_tensor(out=rt[:], in0=st[("ra", first)][:], in1=pos_half[:, 0:2 * count], op=ALU.pow)

        def stage_j(n):
            first, count = unit_of[n]
            if n == first:
                o = work.tile([P, 2 * count, MEM], F32, tag="o%d" % count, name="o", bufs=4)
                st[("o", first)] = o
            o = st[("o", first)]
            eng = nc.vector if scale_on_vector(n) else nc.gpsimd
            for jl in range(2):
                col = 2 * (n - first) + jl
                eng.tensor_scalar(out=o[:, col, :], in0=st[("m", n)][:, jl, :],
                                  scalar1=st[("rt", first)][:, col:col + 1], scalar2=0.0,
                                  op0=ALU.mult, op1=ALU.add)
            if n == first + count - 1:
                nc.sync.dma_start(out=ov[:, 2 * first:2 * (n + 1), :], in_=o[:])

        def ok(n):
            return 0 <= n < NP

        nc.vector.tensor_copy(out=ident_bf[:], in_=ident[:])
        for i in range(-3, NP + 10):
            unit = unit_ending.get(i - 6)
            if i >= 0 and i % 2 == 0 and FIRST_LOADS + i // 2 < len(CHUNKS):
                load_c(FIRST_LOADS + i // 2)
                load_hc(FIRST_LOADS + i // 2)
            if ok(i - 4):
                v3(i - 4)
            if ok(i) and i > 0:
                stage_f(i)
            if ok(i + 1):
                stage_x(i + 1, 0)
            if ok(i + 1) and i >= 0:
                stage_x(i + 1, 1)
            if ok(i - 3) and not in_rows(i - 3):
                stage_h(i - 3)
            if ok(i - 1):
                stage_g(i - 1)
            if unit:
                stat1(*unit)
            if i == 0:
                v1(0)
            if ok(i + 2):
                stage_b(i + 2)
            if i == -2:
                prep_regroup(0)
            if ok(i - 2):
                v2(i - 2)
            if unit:
                stat2(*unit)
            if ok(i) and i > 0:
                v1(i)
            if unit:
                stat3(*unit)
            if ok(i + 2):
                stage_c(i + 2)
            if ok(i) and in_rows(i):
                p2(i)
            if i == -2:
                prep_quant(0)
                prep_bias()
                prep_regroup(1)
            if i == -1:
                prep_quant(1)
                stage_e(0, 0)
                stage_f(0)
                stage_x(0, 1)
            if ok(i + 3):
                stage_a(i + 3)
            if ok(i + 1) and i >= 0:
                stage_e(i + 1, 0)
            if ok(i + 1):
                stage_e(i + 1, 1)
            if ok(i + 3):
                stage_k(i + 3)
            if ok(i - 4):
                stage_sq(i - 4)
            if ok(i + 1) and not in_rows(i + 1):
                stage_hc(i + 1)
            if ok(i - 8) and not scale_on_vector(i - 8):
                stage_j(i - 8)
            if ok(i - 9) and scale_on_vector(i - 9):
                stage_j(i - 9)
            if unit:
                stat4(*unit)
